import numpy as np
import ml_dtypes


def mxq(x, axis, fmt="e4m3"):
    dtype, down = {"e4m3": (ml_dtypes.float8_e4m3fn, 7), "e5m2": (ml_dtypes.float8_e5m2, 14)}[fmt]
    v = np.moveaxis(np.asarray(x, np.float32).astype(ml_dtypes.bfloat16).astype(np.float64), axis, -1)
    blocks = v.reshape(v.shape[:-1] + (-1, 32))
    amax = np.abs(blocks).max(-1, keepdims=True)
    byte = np.maximum(np.where(amax > 0, np.frexp(amax)[1] - 1 + 127, 0) - down, 1)
    scale = np.exp2(byte - 127.0)
    codes = (blocks / scale).astype(np.float32).astype(dtype).astype(np.float64)
    return np.moveaxis((codes * scale).reshape(v.shape), -1, axis)


WIDE = False


def mx_kscale(k):
    if not WIDE:
        return np.ones(k)
    levels = np.array([10, -10, 5, -5, 0])
    if k % 512:
        return np.exp2(np.random.permutation(np.resize(levels, k // 32))).repeat(32)
    a = np.empty((k // 512, 16))
    for p in range(k // 512):
        a[p, :8] = np.random.permutation(np.resize(levels, 8))
        for g in range(8):
            far = levels[np.abs(levels - a[p, g]) >= 10]
            a[p, g + 8] = far[np.random.randint(len(far))]
    return np.exp2(a.ravel()).repeat(32)


BF16 = ml_dtypes.bfloat16


def bf(x):
    return np.asarray(x, np.float32).astype(BF16)


def f64(x):
    return np.asarray(x).astype(np.float64)


B, W, MID = 4096, 256, 1024


def setup_inputs():
    s, t = mx_kscale(MID), mx_kscale(MID)
    return {"h3": bf(np.maximum(np.random.standard_normal((B, MID)), 0.0) * np.sqrt(2.0) * s),
            "w4": bf(np.random.standard_normal((MID, MID)) * np.sqrt(2.0 / MID) / s[:, None] * t),
            "b4": bf(np.random.standard_normal(MID) * 0.1 * t),
            "w5": bf(np.random.standard_normal((MID, W)) * 0.7 / np.sqrt(MID) / t[:, None]),
            "b5": bf(np.random.standard_normal(W) * 0.2),
            "x": bf(np.random.standard_normal((B, W))),
            "log_det_J": bf(np.random.standard_normal(B) * 0.1 * np.sqrt(W))}


def reference(h3, w4, b4, w5, b5, x, log_det_J):
    xf = f64(x)
    x1 = xf[:, 0::2]
    x2 = xf[:, 1::2]
    h4 = np.maximum((mxq(f64(h3), 1, "e4m3") @ mxq(f64(w4), 0, "e4m3")) + f64(b4), 0.0)
    bvec = (mxq(h4, 1, "e4m3") @ mxq(f64(w5), 0, "e4m3")) + f64(b5)
    b1t = np.tanh(bvec[:, 0::2])
    b2t = bvec[:, 1::2]
    y2 = x2 * np.exp(b1t) + b2t
    log_det = f64(log_det_J) + np.sum(b1t, axis=1)
    y = np.stack((x1, y2), axis=2).reshape(xf.shape)
    return (y, log_det)

@@ -1,0 +1,320 @@
+from contextlib import ExitStack
+
+import concourse.mybir as mybir
+from concourse.masks import make_identity
+
+BF16 = mybir.dt.bfloat16
+F32 = mybir.dt.float32
+U32 = mybir.dt.uint32
+U8 = mybir.dt.uint8
+FP8X4 = mybir.dt.float8_e4m3fn_x4
+ACT = mybir.ActivationFunctionType
+ALU = mybir.AluOpType
+
+P = 128
+PACK = 4
+K_PASS = P * PACK
+
+BATCH, MID, WIDTH = 4096, 1024, 256
+HALF = WIDTH // 2
+PASSES = MID // K_PASS
+MID_TILES = MID // P
+TILES = BATCH // P
+GROUP_TILES = 4
+GROUP = GROUP_TILES * P
+GROUPS = TILES // GROUP_TILES
+W4_PIECE = 512
+XT_BANKS, ACC_BANKS, V_BANKS = 3, 3, 2
+
+FLOPS = 2 * BATCH * MID * MID + 2 * BATCH * MID * WIDTH
+
+
+def tile_affinecoupling_pa_t_kernel(tc, h3, w4, b4, w5, b5, x, log_det_J, out_0, out_1):
+    nc = tc.nc
+    with ExitStack() as ctx:
+        keep = ctx.enter_context(tc.tile_pool(name="keep", bufs=1))
+        h3_pool = ctx.enter_context(tc.tile_pool(name="h3_pool", bufs=GROUPS))
+        stage = ctx.enter_context(tc.tile_pool(name="stage", bufs=2))
+        psum = ctx.enter_context(tc.psum_pool(name="psum", bufs=2))
+
+        h3_rows = h3.rearrange("(p t) k -> p t k", t=TILES)
+        x_rows = x.rearrange("(p t) c -> p t c", t=TILES)
+        y_rows = out_0.rearrange("(p t) c -> p t c", t=TILES)
+
+        w4_raw = []
+        for piece in range(MID // W4_PIECE):
+            w4_piece = keep.tile([P, PASSES, PACK, W4_PIECE], BF16, name="w4_raw", bufs=MID // W4_PIECE)
+            w4_raw.append(w4_piece)
+        h3_raw = []
+        for n in range(GROUPS):
+            raw = h3_pool.tile([P, GROUP_TILES, MID], BF16, name="h3_raw")
+            h3_raw.append(raw)
+
+        def load_w4(piece):
+            cols = slice(piece * W4_PIECE, (piece + 1) * W4_PIECE)
+            for g in range(PASSES):
+                nc.sync.dma_start(
+                    out=w4_raw[piece][:, g],
+                    in_=w4[g * K_PASS : (g + 1) * K_PASS, cols].rearrange("(q j) c -> q j c", j=PACK),
+                )
+
+        def load_h3(n):
+            for t in range(GROUP_TILES):
+                nc.sync.dma_start(out=h3_raw[n][:, t, :], in_=h3_rows[:, n * GROUP_TILES + t, :])
+
+        b4_raw = keep.tile([P, PASSES, PACK], BF16)
+        nc.sync.dma_start(out=b4_raw[:], in_=b4.rearrange("(g p j) -> p g j", p=P, j=PACK))
+        x_all = keep.tile([P, TILES, WIDTH], BF16)
+        load_w4(0)
+        load_h3(0)
+        load_w4(1)
+        load_h3(1)
+        load_h3(2)
+        nc.sync.dma_start(out=x_all[:], in_=x_rows)
+        for n in range(3, GROUPS):
+            load_h3(n)
+
+        w5_raw = keep.tile([P, PASSES, PACK, WIDTH], BF16)
+        nc.scalar.dma_start(
+            out=w5_raw[:],
+            in_=w5.rearrange("(g p j) n -> p g j n", j=PACK, p=P),
+        )
+        b5_rows = keep.tile([P, WIDTH], BF16)
+        nc.scalar.dma_start(out=b5_rows[:], in_=b5.partition_broadcast(P))
+        ldj = keep.tile([P, TILES], BF16)
+        nc.scalar.dma_start(out=ldj[:], in_=log_det_J.rearrange("(p t) -> p t", t=TILES))
+
+        warm = keep.tile([P, 1], F32)
+        nc.vector.memset(warm[:], 0.0)
+        nc.scalar.activation(out=warm[:], in_=warm[:], func=ACT.Tanh)
+
+        ident_f32 = keep.tile([P, P], F32)
+        make_identity(nc, ident_f32[:])
+
+        b4_cols = keep.tile([P, MID_TILES], F32)
+        nc.vector.tensor_copy(out=b4_cols[:], in_=b4_raw[:].rearrange("p g j -> p (g j)"))
+
+        w4_codes = keep.tile([P, PASSES, MID], U32, align_bytes=64)
+        w4_scales = keep.tile([P, PASSES, MID], U8, align_bytes=64)
+
+        def pack_w4(piece):
+            cols = slice(piece * W4_PIECE, (piece + 1) * W4_PIECE)
+            grouped = []
+            for g in range(PASSES):
+                w4_grouped = stage.tile([P, W4_PIECE, PACK], BF16, align_bytes=64)
+                nc.vector.tensor_copy(
+                    out=w4_grouped[:].rearrange("p (t m) j -> p t m j", t=PACK),
+                    in_=w4_raw[piece][:, g].rearrange("p j (m t) -> p t m j", t=PACK),
+                )
+                grouped.append(w4_grouped)
+            for g in range(PASSES):
+                nc.vector.quantize_mx(
+                    out=w4_codes[:, g, cols].bitcast(FP8X4),
+                    scales=w4_scales[:, g, cols],
+                    in_=grouped[g][:].rearrange("p c t -> p (c t)"),
+                )
+
+        w5_codes = keep.tile([P, PASSES, WIDTH], U32, align_bytes=64)
+        w5_scales = keep.tile([P, PASSES, WIDTH], U8, align_bytes=64)
+        b5_planes = keep.tile([P, 2, HALF], F32)
+
+        def pack_w5():
+            w5_grouped = keep.tile([P, PASSES, WIDTH, PACK], BF16, align_bytes=64)
+            for g in range(PASSES):
+                nc.vector.tensor_copy(
+                    out=w5_grouped[:, g].rearrange("p (e c) j -> p e c j", e=2),
+                    in_=w5_raw[:, g].rearrange("p j (c e) -> p e c j", e=2),
+                )
+            nc.vector.tensor_copy(out=b5_planes[:], in_=b5_rows[:].rearrange("p (c e) -> p e c", e=2))
+            nc.vector.quantize_mx(
+                out=w5_codes[:].rearrange("p g n -> p (g n)").bitcast(FP8X4),
+                scales=w5_scales[:].rearrange("p g n -> p (g n)"),
+                in_=w5_grouped[:].rearrange("p g n j -> p (g n j)"),
+            )
+
+        live = {}
+        sums = keep.tile([P, TILES], F32)
+
+        def transpose_h3(n):
+            raw_words = h3_raw[n][:].bitcast(F32)
+            h3_grouped = stage.tile([P, PASSES, GROUP, PACK], BF16, align_bytes=64)
+            grouped_words = h3_grouped[:].bitcast(F32)
+            for t in range(GROUP_TILES):
+                xt = psum.tile([P, PASSES * 2, P], F32, tag="xt", bufs=XT_BANKS)
+                for block in range(PASSES * 2):
+                    g, u = divmod(block, 2)
+                    words = slice(g * 2 * P + u, (g + 1) * 2 * P, 2)
+                    nc.tensor.transpose(xt[:, block, :], raw_words[:, t, words], ident_f32[:])
+                nc.scalar.copy(
+                    out=grouped_words[:, :, t * P : (t + 1) * P, :],
+                    in_=xt[:].rearrange("p (g u) r -> p g r u", u=2),
+                )
+            live["h3_grouped", n] = h3_grouped
+
+        def quantise_h3(n):
+            h3_codes = stage.tile([P, PASSES, GROUP], U32, align_bytes=64)
+            h3_scales = stage.tile([P, PASSES, GROUP], U8, align_bytes=64)
+            for g in range(PASSES):
+                nc.vector.quantize_mx(
+                    out=h3_codes[:, g, :].bitcast(FP8X4),
+                    scales=h3_scales[:, g, :],
+                    in_=live["h3_grouped", n][:, g].rearrange("p b t -> p (b t)"),
+                )
+            live["h3_codes", n] = h3_codes
+            live["h3_scales", n] = h3_scales
+
+        def first_matmul(n, g2):
+            if g2 == 0:
+                h4_planes = stage.tile([P, MID_TILES, GROUP], BF16)
+                live["h4_planes", n] = h4_planes
+            for m in range(g2 * PACK, (g2 + 1) * PACK):
+                acc = psum.tile([P, GROUP], F32, tag="acc", bufs=ACC_BANKS)
+                for g in range(PASSES):
+                    nc.tensor.matmul_mx(
+                        out=acc[:],
+                        lhsT=w4_codes[:, g, m * P : (m + 1) * P].bitcast(FP8X4),
+                        lhsT_scale=w4_scales[:, g, m * P : (m + 1) * P],
+                        rhs=live["h3_codes", n][:, g, :].bitcast(FP8X4),
+                        rhs_scale=live["h3_scales", n][:, g, :],
+                        start=(g == 0),
+                        stop=(g == PASSES - 1),
+                    )
+                nc.scalar.activation(
+                    out=live["h4_planes", n][:, m, :],
+                    in_=acc[:],
+                    func=ACT.Relu,
+                    bias=b4_cols[:, m : m + 1],
+                    scale=1.0,
+                )
+
+        def regroup_h4(n, g2):
+            h4_grouped = stage.tile([P, GROUP, PACK], BF16, align_bytes=64)
+            nc.vector.tensor_copy(
+                out=h4_grouped[:].rearrange("p (c i) j -> p c j i", i=4),
+                in_=live["h4_planes", n][:, g2 * PACK : (g2 + 1) * PACK, :].rearrange(
+                    "p j (c i) -> p c j i", i=4
+                ),
+            )
+            live["h4_grouped", n, g2] = h4_grouped
+
+        def quantise_h4(n, g2):
+            if g2 == 0:
+                h4_codes = stage.tile([P, PASSES, GROUP], U32, align_bytes=64)
+                h4_scales = stage.tile([P, PASSES, GROUP], U8, align_bytes=64)
+                live["h4_codes", n] = h4_codes
+                live["h4_scales", n] = h4_scales
+            nc.vector.quantize_mx(
+                out=live["h4_codes", n][:, g2, :].bitcast(FP8X4),
+                scales=live["h4_scales", n][:, g2, :],
+                in_=live["h4_grouped", n, g2][:].rearrange("p b j -> p (b j)"),
+            )
+
+        def second_matmul(n):
+            planes = stage.tile([P, GROUP_TILES, 2, HALF], F32)
+            for pair in range(GROUP_TILES // 2):
+                v = psum.tile([P, 2, WIDTH], F32, tag="v", bufs=V_BANKS)
+                for i in range(2):
+                    rows = slice((2 * pair + i) * P, (2 * pair + i + 1) * P)
+                    for g in range(PASSES):
+                        nc.tensor.matmul_mx(
+                            out=v[:, i, :],
+                            lhsT=live["h4_codes", n][:, g, rows].bitcast(FP8X4),
+                            lhsT_scale=live["h4_scales", n][:, g, rows],
+                            rhs=w5_codes[:, g, :].bitcast(FP8X4),
+                            rhs_scale=w5_scales[:, g, :],
+                            start=(g == 0),
+                            stop=(g == PASSES - 1),
+                        )
+                live["v", n, pair] = v
+            live["planes", n] = planes
+
+        def add_b5(n):
+            for pair in range(GROUP_TILES // 2):
+                nc.vector.tensor_tensor(
+                    out=live["planes", n][:, 2 * pair : 2 * pair + 2].rearrange("p t e c -> p t (e c)"),
+                    in0=live["v", n, pair][:],
+                    in1=b5_planes[:].rearrange("p e c -> p (e c)").unsqueeze(1).to_broadcast([P, 2, WIDTH]),
+                    op=ALU.add,
+                )
+
+        def log_scale(n):
+            ls = stage.tile([P, GROUP_TILES, HALF], F32)
+            for t in range(GROUP_TILES):
+                tile_index = n * GROUP_TILES + t
+                nc.scalar.activation(
+                    out=ls[:, t, :],
+                    in_=live["planes", n][:, t, 0, :],
+                    func=ACT.Tanh,
+                    accum_out=sums[:, tile_index : tile_index + 1],
+                )
+            scale = stage.tile([P, GROUP_TILES, HALF], F32)
+            nc.scalar.activation(out=scale[:], in_=ls[:], func=ACT.Exp)
+            live["scale", n] = scale
+
+        def x_pairs(n):
+            return x_all[:, n * GROUP_TILES : (n + 1) * GROUP_TILES, :].rearrange("p t (c e) -> p t c e", e=2)
+
+        def scale_x(n):
+            nc.vector.tensor_copy(out=live["planes", n][:, :, 0, :], in_=x_pairs(n)[:, :, :, 0])
+            scaled = stage.tile([P, GROUP_TILES, HALF], F32)
+            nc.vector.tensor_tensor(
+                out=scaled[:], in0=x_pairs(n)[:, :, :, 1], in1=live["scale", n][:], op=ALU.mult
+            )
+            live["scaled", n] = scaled
+
+        def shift_x(n):
+            planes = live["planes", n]
+            nc.vector.tensor_tensor(
+                out=planes[:, :, 1, :], in0=planes[:, :, 1, :], in1=live["scaled", n][:], op=ALU.add
+            )
+
+        def store_y(n):
+            y = stage.tile([P, GROUP_TILES, HALF, 2], F32)
+            nc.vector.tensor_copy(out=y[:], in_=live["planes", n][:].rearrange("p t e c -> p t c e"))
+            nc.sync.dma_start(
+                out=y_rows[:, n * GROUP_TILES : (n + 1) * GROUP_TILES, :],
+                in_=y[:].rearrange("p t c e -> p t (c e)"),
+            )
+
+        def on(k):
+            return 0 <= k < GROUPS
+
+        def one_round(n):
+            if on(n - 1):
+                regroup_h4(n - 1, 1)
+            if on(n - 3):
+                shift_x(n - 3)
+            if on(n - 1):
+                quantise_h4(n - 1, 1)
+            if on(n - 3):
+                store_y(n - 3)
+            if on(n):
+                first_matmul(n, 0)
+                regroup_h4(n, 0)
+            if on(n + 1):
+                transpose_h3(n + 1)
+                quantise_h3(n + 1)
+            if on(n):
+                quantise_h4(n, 0)
+            if on(n - 1):
+                second_matmul(n - 1)
+                add_b5(n - 1)
+            if on(n - 2):
+                log_scale(n - 2)
+            if on(n):
+                first_matmul(n, 1)
+            if on(n - 2):
+                scale_x(n - 2)
+
+        pack_w4(0)
+        transpose_h3(0)
+        quantise_h3(0)
+        pack_w4(1)
+        one_round(0)
+        pack_w5()
+        for n in range(1, GROUPS + 3):
+            one_round(n)
+
+        log_det = keep.tile([P, TILES], F32)
+        nc.vector.tensor_tensor(out=log_det[:], in0=sums[:], in1=ldj[:], op=ALU.add)
+        nc.sync.dma_start(out=out_1.rearrange("(p t) -> p t", t=TILES), in_=log_det[:])

@@ -32,6 +32,7 @@ FLOPS = 2 * BATCH * MID * MID + 2 * BATCH * MID * WIDTH
 def tile_affinecoupling_pa_t_kernel(tc, h3, w4, b4, w5, b5, x, log_det_J, out_0, out_1):
     nc = tc.nc
     with ExitStack() as ctx:
+        ctx.enter_context(tc.manual_schedule())
         keep = ctx.enter_context(tc.tile_pool(name="keep", bufs=1))
         h3_pool = ctx.enter_context(tc.tile_pool(name="h3_pool", bufs=GROUPS))
         stage = ctx.enter_context(tc.tile_pool(name="stage", bufs=2))
@@ -65,8 +66,8 @@ def tile_affinecoupling_pa_t_kernel(tc, h3, w4, b4, w5, b5, x, log_det_J, out_0,
         b4_raw = keep.tile([P, PASSES, PACK], BF16)
         nc.sync.dma_start(out=b4_raw[:], in_=b4.rearrange("(g p j) -> p g j", p=P, j=PACK))
         x_all = keep.tile([P, TILES, WIDTH], BF16)
-        load_w4(0)
         load_h3(0)
+        load_w4(0)
         load_w4(1)
         load_h3(1)
         load_h3(2)
@@ -96,23 +97,23 @@ def tile_affinecoupling_pa_t_kernel(tc, h3, w4, b4, w5, b5, x, log_det_J, out_0,
 
         w4_codes = keep.tile([P, PASSES, MID], U32, align_bytes=64)
         w4_scales = keep.tile([P, PASSES, MID], U8, align_bytes=64)
+        live = {}
 
-        def pack_w4(piece):
+        def regroup_w4(piece, g):
+            w4_grouped = stage.tile([P, W4_PIECE, PACK], BF16, align_bytes=64)
+            nc.vector.tensor_copy(
+                out=w4_grouped[:].rearrange("p (t m) j -> p t m j", t=PACK),
+                in_=w4_raw[piece][:, g].rearrange("p j (m t) -> p t m j", t=PACK),
+            )
+            live["w4_grouped", piece, g] = w4_grouped
+
+        def quantise_w4(piece, g):
             cols = slice(piece * W4_PIECE, (piece + 1) * W4_PIECE)
-            grouped = []
-            for g in range(PASSES):
-                w4_grouped = stage.tile([P, W4_PIECE, PACK], BF16, align_bytes=64)
-                nc.vector.tensor_copy(
-                    out=w4_grouped[:].rearrange("p (t m) j -> p t m j", t=PACK),
-                    in_=w4_raw[piece][:, g].rearrange("p j (m t) -> p t m j", t=PACK),
-                )
-                grouped.append(w4_grouped)
-            for g in range(PASSES):
-                nc.vector.quantize_mx(
-                    out=w4_codes[:, g, cols].bitcast(FP8X4),
-                    scales=w4_scales[:, g, cols],
-                    in_=grouped[g][:].rearrange("p c t -> p (c t)"),
-                )
+            nc.vector.quantize_mx(
+                out=w4_codes[:, g, cols].bitcast(FP8X4),
+                scales=w4_scales[:, g, cols],
+                in_=live["w4_grouped", piece, g][:].rearrange("p c t -> p (c t)"),
+            )
 
         w5_codes = keep.tile([P, PASSES, WIDTH], U32, align_bytes=64)
         w5_scales = keep.tile([P, PASSES, WIDTH], U8, align_bytes=64)
@@ -132,14 +133,17 @@ def tile_affinecoupling_pa_t_kernel(tc, h3, w4, b4, w5, b5, x, log_det_J, out_0,
                 in_=w5_grouped[:].rearrange("p g n j -> p (g n j)"),
             )
 
-        live = {}
         sums = keep.tile([P, TILES], F32)
+        ALL = range(GROUP_TILES)
+        PAIRS = (range(0, 2), range(2, GROUP_TILES))
 
-        def transpose_h3(n):
+        def transpose_h3(n, tiles):
+            if tiles[0] == 0:
+                h3_grouped = stage.tile([P, PASSES, GROUP, PACK], BF16, align_bytes=64)
+                live["h3_grouped", n] = h3_grouped
             raw_words = h3_raw[n][:].bitcast(F32)
-            h3_grouped = stage.tile([P, PASSES, GROUP, PACK], BF16, align_bytes=64)
-            grouped_words = h3_grouped[:].bitcast(F32)
-            for t in range(GROUP_TILES):
+            grouped_words = live["h3_grouped", n][:].bitcast(F32)
+            for t in tiles:
                 xt = psum.tile([P, PASSES * 2, P], F32, tag="xt", bufs=XT_BANKS)
                 for block in range(PASSES * 2):
                     g, u = divmod(block, 2)
@@ -149,7 +153,6 @@ def tile_affinecoupling_pa_t_kernel(tc, h3, w4, b4, w5, b5, x, log_det_J, out_0,
                     out=grouped_words[:, :, t * P : (t + 1) * P, :],
                     in_=xt[:].rearrange("p (g u) r -> p g r u", u=2),
                 )
-            live["h3_grouped", n] = h3_grouped
 
         def quantise_h3(n):
             h3_codes = stage.tile([P, PASSES, GROUP], U32, align_bytes=64)
@@ -210,11 +213,10 @@ def tile_affinecoupling_pa_t_kernel(tc, h3, w4, b4, w5, b5, x, log_det_J, out_0,
             )
 
         def second_matmul(n):
-            planes = stage.tile([P, GROUP_TILES, 2, HALF], F32)
-            for pair in range(GROUP_TILES // 2):
+            for pair in PAIRS:
                 v = psum.tile([P, 2, WIDTH], F32, tag="v", bufs=V_BANKS)
-                for i in range(2):
-                    rows = slice((2 * pair + i) * P, (2 * pair + i + 1) * P)
+                for i, t in enumerate(pair):
+                    rows = slice(t * P, (t + 1) * P)
                     for g in range(PASSES):
                         nc.tensor.matmul_mx(
                             out=v[:, i, :],
@@ -226,94 +228,140 @@ def tile_affinecoupling_pa_t_kernel(tc, h3, w4, b4, w5, b5, x, log_det_J, out_0,
                             stop=(g == PASSES - 1),
                         )
                 live["v", n, pair] = v
-            live["planes", n] = planes
-
-        def add_b5(n):
-            for pair in range(GROUP_TILES // 2):
-                nc.vector.tensor_tensor(
-                    out=live["planes", n][:, 2 * pair : 2 * pair + 2].rearrange("p t e c -> p t (e c)"),
-                    in0=live["v", n, pair][:],
-                    in1=b5_planes[:].rearrange("p e c -> p (e c)").unsqueeze(1).to_broadcast([P, 2, WIDTH]),
-                    op=ALU.add,
-                )
-
-        def log_scale(n):
+            planes = stage.tile([P, GROUP_TILES, 2, HALF], F32)
             ls = stage.tile([P, GROUP_TILES, HALF], F32)
-            for t in range(GROUP_TILES):
+            scale = stage.tile([P, GROUP_TILES, HALF], F32)
+            scaled = stage.tile([P, GROUP_TILES, HALF], F32)
+            y = stage.tile([P, GROUP_TILES, HALF, 2], F32)
+            live["coupling", n] = planes, ls, scale, scaled, y
+
+        def part(tile, tiles):
+            return tile[:, tiles.start : tiles.stop]
+
+        def x_pairs(n, tiles):
+            first = n * GROUP_TILES
+            return x_all[:, first + tiles.start : first + tiles.stop, :].rearrange("p t (c e) -> p t c e", e=2)
+
+        def add_b5(n, pair):
+            planes = live["coupling", n][0]
+            nc.vector.tensor_tensor(
+                out=part(planes, pair).rearrange("p t e c -> p t (e c)"),
+                in0=live["v", n, pair][:],
+                in1=b5_planes[:].rearrange("p e c -> p (e c)").unsqueeze(1).to_broadcast([P, 2, WIDTH]),
+                op=ALU.add,
+            )
+
+        def log_scale(n, tiles):
+            planes, ls, scale, scaled, y = live["coupling", n]
+            for t in tiles:
                 tile_index = n * GROUP_TILES + t
                 nc.scalar.activation(
                     out=ls[:, t, :],
-                    in_=live["planes", n][:, t, 0, :],
+                    in_=planes[:, t, 0, :],
                     func=ACT.Tanh,
                     accum_out=sums[:, tile_index : tile_index + 1],
                 )
-            scale = stage.tile([P, GROUP_TILES, HALF], F32)
-            nc.scalar.activation(out=scale[:], in_=ls[:], func=ACT.Exp)
-            live["scale", n] = scale
+            nc.scalar.activation(out=part(scale, tiles), in_=part(ls, tiles), func=ACT.Exp)
 
-        def x_pairs(n):
-            return x_all[:, n * GROUP_TILES : (n + 1) * GROUP_TILES, :].rearrange("p t (c e) -> p t c e", e=2)
-
-        def scale_x(n):
-            nc.vector.tensor_copy(out=live["planes", n][:, :, 0, :], in_=x_pairs(n)[:, :, :, 0])
-            scaled = stage.tile([P, GROUP_TILES, HALF], F32)
+        def scale_x(n, tiles):
+            planes, ls, scale, scaled, y = live["coupling", n]
             nc.vector.tensor_tensor(
-                out=scaled[:], in0=x_pairs(n)[:, :, :, 1], in1=live["scale", n][:], op=ALU.mult
-            )
-            live["scaled", n] = scaled
-
-        def shift_x(n):
-            planes = live["planes", n]
-            nc.vector.tensor_tensor(
-                out=planes[:, :, 1, :], in0=planes[:, :, 1, :], in1=live["scaled", n][:], op=ALU.add
+                out=part(scaled, tiles), in0=x_pairs(n, tiles)[:, :, :, 1], in1=part(scale, tiles), op=ALU.mult
             )
 
-        def store_y(n):
-            y = stage.tile([P, GROUP_TILES, HALF, 2], F32)
-            nc.vector.tensor_copy(out=y[:], in_=live["planes", n][:].rearrange("p t e c -> p t c e"))
+        def pass_x(n, tiles):
+            planes = live["coupling", n][0]
+            nc.vector.tensor_copy(out=part(planes, tiles)[:, :, 0, :], in_=x_pairs(n, tiles)[:, :, :, 0])
+
+        def shift_x(n, tiles):
+            planes, ls, scale, scaled, y = live["coupling", n]
+            shifted = part(planes, tiles)[:, :, 1, :]
+            nc.vector.tensor_tensor(out=shifted, in0=shifted, in1=part(scaled, tiles), op=ALU.add)
+
+        def store_y(n, tiles):
+            planes, ls, scale, scaled, y = live["coupling", n]
+            nc.vector.tensor_copy(out=part(y, tiles), in_=part(planes, tiles).rearrange("p t e c -> p t c e"))
+            first = n * GROUP_TILES
             nc.sync.dma_start(
-                out=y_rows[:, n * GROUP_TILES : (n + 1) * GROUP_TILES, :],
-                in_=y[:].rearrange("p t c e -> p t (c e)"),
+                out=y_rows[:, first + tiles.start : first + tiles.stop, :],
+                in_=part(y, tiles).rearrange("p t c e -> p t (c e)"),
             )
 
         def on(k):
             return 0 <= k < GROUPS
 
         def one_round(n):
+            if on(n):
+                first_matmul(n, 0)
+            if on(n - 3):
+                shift_x(n - 3, ALL)
+                pass_x(n - 3, ALL)
             if on(n - 1):
                 regroup_h4(n - 1, 1)
             if on(n - 3):
-                shift_x(n - 3)
+                store_y(n - 3, ALL)
             if on(n - 1):
                 quantise_h4(n - 1, 1)
-            if on(n - 3):
-                store_y(n - 3)
-            if on(n):
-                first_matmul(n, 0)
-                regroup_h4(n, 0)
             if on(n + 1):
-                transpose_h3(n + 1)
-                quantise_h3(n + 1)
+                transpose_h3(n + 1, PAIRS[0])
+            if on(n - 1):
+                second_matmul(n - 1)
+            if on(n - 2):
+                log_scale(n - 2, ALL)
+            if on(n + 1):
+                transpose_h3(n + 1, PAIRS[1])
+            if on(n):
+                regroup_h4(n, 0)
+            if on(n - 1):
+                add_b5(n - 1, PAIRS[0])
             if on(n):
                 quantise_h4(n, 0)
             if on(n - 1):
-                second_matmul(n - 1)
-                add_b5(n - 1)
+                add_b5(n - 1, PAIRS[1])
             if on(n - 2):
-                log_scale(n - 2)
+                scale_x(n - 2, ALL)
+            if on(n + 1):
+                quantise_h3(n + 1)
             if on(n):
                 first_matmul(n, 1)
-            if on(n - 2):
-                scale_x(n - 2)
 
-        pack_w4(0)
-        transpose_h3(0)
+        def last_round():
+            n = GROUPS - 1
+            regroup_h4(n, 1)
+            shift_x(n - 2, ALL)
+            quantise_h4(n, 1)
+            log_scale(n - 1, ALL)
+            second_matmul(n)
+            pass_x(n - 2, ALL)
+            store_y(n - 2, ALL)
+            scale_x(n - 1, ALL)
+            pass_x(n - 1, ALL)
+            shift_x(n - 1, ALL)
+            for pair in PAIRS:
+                add_b5(n, pair)
+                log_scale(n, pair)
+            store_y(n - 1, ALL)
+            for pair in PAIRS:
+                scale_x(n, pair)
+                pass_x(n, pair)
+                shift_x(n, pair)
+                store_y(n, pair)
+
+        transpose_h3(0, ALL)
+        regroup_w4(0, 0)
+        regroup_w4(0, 1)
+        quantise_w4(0, 0)
+        quantise_w4(0, 1)
         quantise_h3(0)
-        pack_w4(1)
+        regroup_w4(1, 0)
+        regroup_w4(1, 1)
+        quantise_w4(1, 0)
+        quantise_w4(1, 1)
         one_round(0)
         pack_w5()
-        for n in range(1, GROUPS + 3):
+        for n in range(1, GROUPS):
             one_round(n)
+        last_round()
 
         log_det = keep.tile([P, TILES], F32)
         nc.vector.tensor_tensor(out=log_det[:], in0=sums[:], in1=ldj[:], op=ALU.add)

@@ -63,27 +63,24 @@ def tile_affinecoupling_pa_t_kernel(tc, h3, w4, b4, w5, b5, x, log_det_J, out_0,
             for t in range(GROUP_TILES):
                 nc.sync.dma_start(out=h3_raw[n][:, t, :], in_=h3_rows[:, n * GROUP_TILES + t, :])
 
-        b4_raw = keep.tile([P, PASSES, PACK], BF16)
-        nc.sync.dma_start(out=b4_raw[:], in_=b4.rearrange("(g p j) -> p g j", p=P, j=PACK))
+        bias_rows = keep.tile([P, MID + WIDTH], BF16)
+        nc.vector.memset(bias_rows[:], 0.0)
+        nc.scalar.dma_start(out=bias_rows[0:1, 0:MID], in_=b4.rearrange("(o k) -> o k", o=1))
+        nc.scalar.dma_start(out=bias_rows[0:1, MID : MID + WIDTH], in_=b5.rearrange("(o k) -> o k", o=1))
+
+        w5_raw = keep.tile([P, PASSES, PACK, WIDTH], BF16)
         x_all = keep.tile([P, TILES, WIDTH], BF16)
-        load_h3(0)
+        ldj = keep.tile([P, TILES], BF16)
         load_w4(0)
+        load_h3(0)
         load_w4(1)
         load_h3(1)
+        nc.sync.dma_start(out=w5_raw[:], in_=w5.rearrange("(g p j) n -> p g j n", j=PACK, p=P))
         load_h3(2)
         nc.sync.dma_start(out=x_all[:], in_=x_rows)
         for n in range(3, GROUPS):
             load_h3(n)
-
-        w5_raw = keep.tile([P, PASSES, PACK, WIDTH], BF16)
-        nc.scalar.dma_start(
-            out=w5_raw[:],
-            in_=w5.rearrange("(g p j) n -> p g j n", j=PACK, p=P),
-        )
-        b5_rows = keep.tile([P, WIDTH], BF16)
-        nc.scalar.dma_start(out=b5_rows[:], in_=b5.partition_broadcast(P))
-        ldj = keep.tile([P, TILES], BF16)
-        nc.scalar.dma_start(out=ldj[:], in_=log_det_J.rearrange("(p t) -> p t", t=TILES))
+        nc.sync.dma_start(out=ldj[:], in_=log_det_J.rearrange("(p t) -> p t", t=TILES))
 
         warm = keep.tile([P, 1], F32)
         nc.vector.memset(warm[:], 0.0)
@@ -92,8 +89,39 @@ def tile_affinecoupling_pa_t_kernel(tc, h3, w4, b4, w5, b5, x, log_det_J, out_0,
         ident_f32 = keep.tile([P, P], F32)
         make_identity(nc, ident_f32[:])
 
+        ones = keep.tile([P, P], BF16)
+        nc.vector.memset(ones[:], 1.0)
         b4_cols = keep.tile([P, MID_TILES], F32)
-        nc.vector.tensor_copy(out=b4_cols[:], in_=b4_raw[:].rearrange("p g j -> p (g j)"))
+        b5_planes = keep.tile([P, 2, HALF], F32)
+
+        def spread_biases():
+            spread = psum.tile([P, WIDTH + MID_TILES], F32, tag="v", bufs=V_BANKS)
+            nc.tensor.matmul(
+                spread[:, 0:WIDTH],
+                lhsT=ones[:],
+                rhs=bias_rows[:, MID : MID + WIDTH].rearrange("p (c e) -> p e c", e=2),
+                start=True,
+                stop=True,
+            )
+            for m in range(MID_TILES):
+                g, j = divmod(m, PACK)
+                nc.tensor.matmul(
+                    spread[:, WIDTH + m : WIDTH + m + 1],
+                    lhsT=bias_rows[:, g * K_PASS + j : (g + 1) * K_PASS : PACK],
+                    rhs=ones[:, 0:1],
+                    start=True,
+                    stop=True,
+                )
+            nc.vector.tensor_copy(out=b4_cols[:], in_=spread[:, WIDTH : WIDTH + MID_TILES])
+            nc.vector.tensor_copy(out=b5_planes[:].rearrange("p e c -> p (e c)"), in_=spread[:, 0:WIDTH])
+
+        zeros = keep.tile([P, GROUP], BF16)
+        nc.vector.memset(zeros[:], 0.0)
+
+        def warm_up(matmuls):
+            idle = psum.tile([P, GROUP], F32, tag="acc", bufs=ACC_BANKS)
+            for i in range(matmuls):
+                nc.tensor.matmul(idle[:], lhsT=zeros[:, 0:P], rhs=zeros[:], start=True, stop=True)
 
         w4_codes = keep.tile([P, PASSES, MID], U32, align_bytes=64)
         w4_scales = keep.tile([P, PASSES, MID], U8, align_bytes=64)
@@ -117,7 +145,6 @@ def tile_affinecoupling_pa_t_kernel(tc, h3, w4, b4, w5, b5, x, log_det_J, out_0,
 
         w5_codes = keep.tile([P, PASSES, WIDTH], U32, align_bytes=64)
         w5_scales = keep.tile([P, PASSES, WIDTH], U8, align_bytes=64)
-        b5_planes = keep.tile([P, 2, HALF], F32)
 
         def pack_w5():
             w5_grouped = keep.tile([P, PASSES, WIDTH, PACK], BF16, align_bytes=64)
@@ -126,7 +153,6 @@ def tile_affinecoupling_pa_t_kernel(tc, h3, w4, b4, w5, b5, x, log_det_J, out_0,
                     out=w5_grouped[:, g].rearrange("p (e c) j -> p e c j", e=2),
                     in_=w5_raw[:, g].rearrange("p j (c e) -> p e c j", e=2),
                 )
-            nc.vector.tensor_copy(out=b5_planes[:], in_=b5_rows[:].rearrange("p (c e) -> p e c", e=2))
             nc.vector.quantize_mx(
                 out=w5_codes[:].rearrange("p g n -> p (g n)").bitcast(FP8X4),
                 scales=w5_scales[:].rearrange("p g n -> p (g n)"),
@@ -347,11 +373,15 @@ def tile_affinecoupling_pa_t_kernel(tc, h3, w4, b4, w5, b5, x, log_det_J, out_0,
                 shift_x(n, pair)
                 store_y(n, pair)
 
-        transpose_h3(0, ALL)
+        warm_up(4)
+        spread_biases()
+        warm_up(4)
         regroup_w4(0, 0)
         regroup_w4(0, 1)
         quantise_w4(0, 0)
         quantise_w4(0, 1)
+        transpose_h3(0, ALL)
+        warm_up(5)
         quantise_h3(0)
         regroup_w4(1, 0)
         regroup_w4(1, 1)

@@ -24,7 +24,7 @@ GROUP_TILES = 4
 GROUP = GROUP_TILES * P
 GROUPS = TILES // GROUP_TILES
 W4_PIECE = 512
-XT_BANKS, ACC_BANKS, V_BANKS = 3, 3, 2
+BANKS = 8
 
 FLOPS = 2 * BATCH * MID * MID + 2 * BATCH * MID * WIDTH
 
@@ -64,7 +64,7 @@ def tile_affinecoupling_pa_t_kernel(tc, h3, w4, b4, w5, b5, x, log_det_J, out_0,
                 nc.sync.dma_start(out=h3_raw[n][:, t, :], in_=h3_rows[:, n * GROUP_TILES + t, :])
 
         bias_rows = keep.tile([P, MID + WIDTH], BF16)
-        nc.vector.memset(bias_rows[:], 0.0)
+        nc.gpsimd.memset(bias_rows[:], 0.0)
         nc.scalar.dma_start(out=bias_rows[0:1, 0:MID], in_=b4.rearrange("(o k) -> o k", o=1))
         nc.scalar.dma_start(out=bias_rows[0:1, MID : MID + WIDTH], in_=b5.rearrange("(o k) -> o k", o=1))
 
@@ -95,7 +95,7 @@ def tile_affinecoupling_pa_t_kernel(tc, h3, w4, b4, w5, b5, x, log_det_J, out_0,
         b5_planes = keep.tile([P, 2, HALF], F32)
 
         def spread_biases():
-            spread = psum.tile([P, WIDTH + MID_TILES], F32, tag="v", bufs=V_BANKS)
+            spread = psum.tile([P, WIDTH + MID_TILES], F32, tag="bank", bufs=BANKS)
             nc.tensor.matmul(
                 spread[:, 0:WIDTH],
                 lhsT=ones[:],
@@ -112,6 +112,10 @@ def tile_affinecoupling_pa_t_kernel(tc, h3, w4, b4, w5, b5, x, log_det_J, out_0,
                     start=True,
                     stop=True,
                 )
+            live["spread"] = spread
+
+        def keep_biases():
+            spread = live["spread"]
             nc.vector.tensor_copy(out=b4_cols[:], in_=spread[:, WIDTH : WIDTH + MID_TILES])
             nc.vector.tensor_copy(out=b5_planes[:].rearrange("p e c -> p (e c)"), in_=spread[:, 0:WIDTH])
 
@@ -119,14 +123,14 @@ def tile_affinecoupling_pa_t_kernel(tc, h3, w4, b4, w5, b5, x, log_det_J, out_0,
         nc.vector.memset(zeros[:], 0.0)
 
         def warm_up(matmuls):
-            idle = psum.tile([P, GROUP], F32, tag="acc", bufs=ACC_BANKS)
+            idle = psum.tile([P, GROUP], F32, tag="bank", bufs=BANKS)
             for i in range(matmuls):
                 nc.tensor.matmul(idle[:], lhsT=zeros[:, 0:P], rhs=zeros[:], start=True, stop=True)
 
-        w4_codes = keep.tile([P, PASSES, MID], U32, align_bytes=64)
-        w4_scales = keep.tile([P, PASSES, MID], U8, align_bytes=64)
         live = {}
 
+        w4_codes = keep.tile([P, PASSES, MID], U32, align_bytes=64)
+        w4_scales = keep.tile([P, PASSES, MID], U8, align_bytes=64)
         def regroup_w4(piece, g):
             w4_grouped = stage.tile([P, W4_PIECE, PACK], BF16, align_bytes=64)
             nc.vector.tensor_copy(
@@ -170,7 +174,7 @@ def tile_affinecoupling_pa_t_kernel(tc, h3, w4, b4, w5, b5, x, log_det_J, out_0,
             raw_words = h3_raw[n][:].bitcast(F32)
             grouped_words = live["h3_grouped", n][:].bitcast(F32)
             for t in tiles:
-                xt = psum.tile([P, PASSES * 2, P], F32, tag="xt", bufs=XT_BANKS)
+                xt = psum.tile([P, PASSES * 2, P], F32, tag="bank", bufs=BANKS)
                 for block in range(PASSES * 2):
                     g, u = divmod(block, 2)
                     words = slice(g * 2 * P + u, (g + 1) * 2 * P, 2)
@@ -197,7 +201,7 @@ def tile_affinecoupling_pa_t_kernel(tc, h3, w4, b4, w5, b5, x, log_det_J, out_0,
                 h4_planes = stage.tile([P, MID_TILES, GROUP], BF16)
                 live["h4_planes", n] = h4_planes
             for m in range(g2 * PACK, (g2 + 1) * PACK):
-                acc = psum.tile([P, GROUP], F32, tag="acc", bufs=ACC_BANKS)
+                acc = psum.tile([P, GROUP], F32, tag="bank", bufs=BANKS)
                 for g in range(PASSES):
                     nc.tensor.matmul_mx(
                         out=acc[:],
@@ -240,7 +244,7 @@ def tile_affinecoupling_pa_t_kernel(tc, h3, w4, b4, w5, b5, x, log_det_J, out_0,
 
         def second_matmul(n):
             for pair in PAIRS:
-                v = psum.tile([P, 2, WIDTH], F32, tag="v", bufs=V_BANKS)
+                v = psum.tile([P, 2, WIDTH], F32, tag="bank", bufs=BANKS)
                 for i, t in enumerate(pair):
                     rows = slice(t * P, (t + 1) * P)
                     for g in range(PASSES):
@@ -382,6 +386,7 @@ def tile_affinecoupling_pa_t_kernel(tc, h3, w4, b4, w5, b5, x, log_det_J, out_0,
         quantise_w4(0, 1)
         transpose_h3(0, ALL)
         warm_up(5)
+        keep_biases()
         quantise_h3(0)
         regroup_w4(1, 0)
         regroup_w4(1, 1)

@@ -377,17 +377,16 @@ def tile_affinecoupling_pa_t_kernel(tc, h3, w4, b4, w5, b5, x, log_det_J, out_0,
                 shift_x(n, pair)
                 store_y(n, pair)
 
-        warm_up(4)
-        spread_biases()
-        warm_up(4)
+        warm_up(6)
         regroup_w4(0, 0)
         regroup_w4(0, 1)
         quantise_w4(0, 0)
         quantise_w4(0, 1)
         transpose_h3(0, ALL)
-        warm_up(5)
-        keep_biases()
+        spread_biases()
+        warm_up(4)
         quantise_h3(0)
+        keep_biases()
         regroup_w4(1, 0)
         regroup_w4(1, 1)
         quantise_w4(1, 0)

@@ -34,7 +34,7 @@ def tile_affinecoupling_pa_t_kernel(tc, h3, w4, b4, w5, b5, x, log_det_J, out_0,
     with ExitStack() as ctx:
         ctx.enter_context(tc.manual_schedule())
         keep = ctx.enter_context(tc.tile_pool(name="keep", bufs=1))
-        h3_pool = ctx.enter_context(tc.tile_pool(name="h3_pool", bufs=GROUPS))
+        h3_pool = ctx.enter_context(tc.tile_pool(name="h3_pool", bufs=GROUPS - 1))
         stage = ctx.enter_context(tc.tile_pool(name="stage", bufs=2))
         psum = ctx.enter_context(tc.psum_pool(name="psum", bufs=2))
 
@@ -167,32 +167,41 @@ def tile_affinecoupling_pa_t_kernel(tc, h3, w4, b4, w5, b5, x, log_det_J, out_0,
         ALL = range(GROUP_TILES)
         PAIRS = (range(0, 2), range(2, GROUP_TILES))
 
-        def transpose_h3(n, tiles):
-            if tiles[0] == 0:
-                h3_grouped = stage.tile([P, PASSES, GROUP, PACK], BF16, align_bytes=64)
-                live["h3_grouped", n] = h3_grouped
+        def vector_tiles(n):
+            return range(n % 2)
+
+        def transpose_h3(n):
+            h3_grouped = stage.tile([P, PASSES, GROUP, PACK], BF16, align_bytes=64, bufs=3)
+            live["h3_grouped", n] = h3_grouped
             raw_words = h3_raw[n][:].bitcast(F32)
-            grouped_words = live["h3_grouped", n][:].bitcast(F32)
-            for t in tiles:
+            for t in range(GROUP_TILES):
                 xt = psum.tile([P, PASSES * 2, P], F32, tag="bank", bufs=BANKS)
                 for block in range(PASSES * 2):
                     g, u = divmod(block, 2)
                     words = slice(g * 2 * P + u, (g + 1) * 2 * P, 2)
                     nc.tensor.transpose(xt[:, block, :], raw_words[:, t, words], ident_f32[:])
-                nc.scalar.copy(
-                    out=grouped_words[:, :, t * P : (t + 1) * P, :],
-                    in_=xt[:].rearrange("p (g u) r -> p g r u", u=2),
-                )
+                live["xt", n, t] = xt
+                if t not in vector_tiles(n):
+                    empty_xt(n, t, nc.scalar.copy)
+
+        def empty_xt(n, t, copy):
+            copy(
+                out=live["h3_grouped", n][:].bitcast(F32)[:, :, t * P : (t + 1) * P, :],
+                in_=live["xt", n, t][:].rearrange("p (g u) r -> p g r u", u=2),
+            )
+
+        def empty_vector_tiles(n):
+            for t in vector_tiles(n):
+                empty_xt(n, t, nc.vector.tensor_copy)
 
         def quantise_h3(n):
             h3_codes = stage.tile([P, PASSES, GROUP], U32, align_bytes=64)
             h3_scales = stage.tile([P, PASSES, GROUP], U8, align_bytes=64)
-            for g in range(PASSES):
-                nc.vector.quantize_mx(
-                    out=h3_codes[:, g, :].bitcast(FP8X4),
-                    scales=h3_scales[:, g, :],
-                    in_=live["h3_grouped", n][:, g].rearrange("p b t -> p (b t)"),
-                )
+            nc.vector.quantize_mx(
+                out=h3_codes[:].rearrange("p g b -> p (g b)").bitcast(FP8X4),
+                scales=h3_scales[:].rearrange("p g b -> p (g b)"),
+                in_=live["h3_grouped", n][:].rearrange("p g b t -> p (g b t)"),
+            )
             live["h3_codes", n] = h3_codes
             live["h3_scales", n] = h3_scales
 
@@ -262,8 +271,7 @@ def tile_affinecoupling_pa_t_kernel(tc, h3, w4, b4, w5, b5, x, log_det_J, out_0,
             ls = stage.tile([P, GROUP_TILES, HALF], F32)
             scale = stage.tile([P, GROUP_TILES, HALF], F32)
             scaled = stage.tile([P, GROUP_TILES, HALF], F32)
-            y = stage.tile([P, GROUP_TILES, HALF, 2], F32)
-            live["coupling", n] = planes, ls, scale, scaled, y
+            live["coupling", n] = planes, ls, scale, scaled
 
         def part(tile, tiles):
             return tile[:, tiles.start : tiles.stop]
@@ -282,7 +290,7 @@ def tile_affinecoupling_pa_t_kernel(tc, h3, w4, b4, w5, b5, x, log_det_J, out_0,
             )
 
         def log_scale(n, tiles):
-            planes, ls, scale, scaled, y = live["coupling", n]
+            planes, ls, scale, scaled = live["coupling", n]
             for t in tiles:
                 tile_index = n * GROUP_TILES + t
                 nc.scalar.activation(
@@ -294,23 +302,41 @@ def tile_affinecoupling_pa_t_kernel(tc, h3, w4, b4, w5, b5, x, log_det_J, out_0,
             nc.scalar.activation(out=part(scale, tiles), in_=part(ls, tiles), func=ACT.Exp)
 
         def scale_x(n, tiles):
-            planes, ls, scale, scaled, y = live["coupling", n]
+            planes, ls, scale, scaled = live["coupling", n]
             nc.vector.tensor_tensor(
                 out=part(scaled, tiles), in0=x_pairs(n, tiles)[:, :, :, 1], in1=part(scale, tiles), op=ALU.mult
             )
 
-        def pass_x(n, tiles):
-            planes = live["coupling", n][0]
-            nc.vector.tensor_copy(out=part(planes, tiles)[:, :, 0, :], in_=x_pairs(n, tiles)[:, :, :, 0])
+        def pass_x(n):
+            y_planes = stage.tile([P, GROUP_TILES, 2, HALF], F32)
+            live["y_planes", n] = y_planes
+            nc.gpsimd.tensor_scalar(
+                out=y_planes[:, :, 0, :],
+                in0=x_pairs(n, ALL)[:, :, :, 0],
+                scalar1=1.0,
+                scalar2=0.0,
+                op0=ALU.mult,
+                op1=ALU.add,
+            )
 
         def shift_x(n, tiles):
-            planes, ls, scale, scaled, y = live["coupling", n]
-            shifted = part(planes, tiles)[:, :, 1, :]
-            nc.vector.tensor_tensor(out=shifted, in0=shifted, in1=part(scaled, tiles), op=ALU.add)
+            planes, ls, scale, scaled = live["coupling", n]
+            nc.vector.tensor_tensor(
+                out=part(live["y_planes", n], tiles)[:, :, 1, :],
+                in0=part(planes, tiles)[:, :, 1, :],
+                in1=part(scaled, tiles),
+                op=ALU.add,
+            )
 
-        def store_y(n, tiles):
-            planes, ls, scale, scaled, y = live["coupling", n]
-            nc.vector.tensor_copy(out=part(y, tiles), in_=part(planes, tiles).rearrange("p t e c -> p t c e"))
+        def interleave_on_gpsimd(out, in_):
+            nc.gpsimd.tensor_scalar(out=out, in0=in_, scalar1=1.0, scalar2=0.0, op0=ALU.mult, op1=ALU.add)
+
+        def store_y(n, tiles, interleave):
+            if tiles.start == 0:
+                y = stage.tile([P, GROUP_TILES, HALF, 2], F32)
+                live["y", n] = y
+            y = live["y", n]
+            interleave(out=part(y, tiles), in_=part(live["y_planes", n], tiles).rearrange("p t e c -> p t c e"))
             first = n * GROUP_TILES
             nc.sync.dma_start(
                 out=y_rows[:, first + tiles.start : first + tiles.stop, :],
@@ -321,68 +347,85 @@ def tile_affinecoupling_pa_t_kernel(tc, h3, w4, b4, w5, b5, x, log_det_J, out_0,
             return 0 <= k < GROUPS
 
         def one_round(n):
-            if on(n):
-                first_matmul(n, 0)
-            if on(n - 3):
-                shift_x(n - 3, ALL)
-                pass_x(n - 3, ALL)
+            first_matmul(n, 0)
+            if n == 0:
+                transpose_h3(1)
+            first_matmul(n, 1)
+            if n == 0:
+                empty_vector_tiles(1)
+                pack_w5()
             if on(n - 1):
                 regroup_h4(n - 1, 1)
             if on(n - 3):
-                store_y(n - 3, ALL)
+                scale_x(n - 3, ALL)
             if on(n - 1):
                 quantise_h4(n - 1, 1)
-            if on(n + 1):
-                transpose_h3(n + 1, PAIRS[0])
+            quantise_h3(n + 1)
+            regroup_h4(n, 0)
             if on(n - 1):
                 second_matmul(n - 1)
             if on(n - 2):
                 log_scale(n - 2, ALL)
-            if on(n + 1):
-                transpose_h3(n + 1, PAIRS[1])
-            if on(n):
-                regroup_h4(n, 0)
+            if on(n + 2):
+                transpose_h3(n + 2)
+            if on(n - 3):
+                shift_x(n - 3, ALL)
+                store_y(n - 3, ALL, interleave_on_gpsimd)
+                pass_x(n - 2)
             if on(n - 1):
-                add_b5(n - 1, PAIRS[0])
-            if on(n):
-                quantise_h4(n, 0)
-            if on(n - 1):
-                add_b5(n - 1, PAIRS[1])
-            if on(n - 2):
-                scale_x(n - 2, ALL)
-            if on(n + 1):
-                quantise_h3(n + 1)
-            if on(n):
-                first_matmul(n, 1)
+                for pair in PAIRS:
+                    add_b5(n - 1, pair)
+            if on(n + 2):
+                empty_vector_tiles(n + 2)
+            quantise_h4(n, 0)
 
-        def last_round():
+        def last_rounds():
             n = GROUPS - 1
+            first_matmul(n, 0)
+            regroup_h4(n - 1, 1)
+            scale_x(n - 3, ALL)
+            quantise_h4(n - 1, 1)
+            first_matmul(n, 1)
+            second_matmul(n - 1)
+            log_scale(n - 2, ALL)
+            regroup_h4(n, 0)
+            shift_x(n - 3, ALL)
+            store_y(n - 3, ALL, interleave_on_gpsimd)
+            pass_x(n - 2)
+            quantise_h4(n, 0)
             regroup_h4(n, 1)
-            shift_x(n - 2, ALL)
+            add_b5(n - 1, PAIRS[0])
             quantise_h4(n, 1)
-            log_scale(n - 1, ALL)
             second_matmul(n)
-            pass_x(n - 2, ALL)
-            store_y(n - 2, ALL)
-            scale_x(n - 1, ALL)
-            pass_x(n - 1, ALL)
-            shift_x(n - 1, ALL)
+            add_b5(n - 1, PAIRS[1])
+            log_scale(n - 1, ALL)
+            scale_x(n - 2, ALL)
+            pass_x(n - 1)
+            shift_x(n - 2, ALL)
+            store_y(n - 2, ALL, nc.scalar.copy)
             for pair in PAIRS:
                 add_b5(n, pair)
-                log_scale(n, pair)
-            store_y(n - 1, ALL)
             for pair in PAIRS:
-                scale_x(n, pair)
-                pass_x(n, pair)
-                shift_x(n, pair)
-                store_y(n, pair)
+                log_scale(n, pair)
+            scale_x(n - 1, ALL)
+            shift_x(n - 1, ALL)
+            pass_x(n)
+            scale_x(n, PAIRS[0])
+            store_y(n - 1, ALL, nc.vector.tensor_copy)
+            shift_x(n, PAIRS[0])
+            scale_x(n, PAIRS[1])
+            store_y(n, PAIRS[0], nc.vector.tensor_copy)
+            shift_x(n, PAIRS[1])
+            store_y(n, PAIRS[1], nc.vector.tensor_copy)
 
+        pass_x(0)
         warm_up(6)
         regroup_w4(0, 0)
         regroup_w4(0, 1)
         quantise_w4(0, 0)
         quantise_w4(0, 1)
-        transpose_h3(0, ALL)
+        transpose_h3(0)
+        empty_vector_tiles(0)
         spread_biases()
         warm_up(4)
         quantise_h3(0)
@@ -391,11 +434,9 @@ def tile_affinecoupling_pa_t_kernel(tc, h3, w4, b4, w5, b5, x, log_det_J, out_0,
         regroup_w4(1, 1)
         quantise_w4(1, 0)
         quantise_w4(1, 1)
-        one_round(0)
-        pack_w5()
-        for n in range(1, GROUPS):
+        for n in range(GROUPS - 1):
             one_round(n)
-        last_round()
+        last_rounds()
 
         log_det = keep.tile([P, TILES], F32)
         nc.vector.tensor_tensor(out=log_det[:], in0=sums[:], in1=ldj[:], op=ALU.add)

@@ -34,7 +34,7 @@ def tile_affinecoupling_pa_t_kernel(tc, h3, w4, b4, w5, b5, x, log_det_J, out_0,
     with ExitStack() as ctx:
         ctx.enter_context(tc.manual_schedule())
         keep = ctx.enter_context(tc.tile_pool(name="keep", bufs=1))
-        h3_pool = ctx.enter_context(tc.tile_pool(name="h3_pool", bufs=GROUPS - 1))
+        h3_pool = ctx.enter_context(tc.tile_pool(name="h3_pool", bufs=GROUPS - 2))
         stage = ctx.enter_context(tc.tile_pool(name="stage", bufs=2))
         psum = ctx.enter_context(tc.psum_pool(name="psum", bufs=2))
 
@@ -129,8 +129,8 @@ def tile_affinecoupling_pa_t_kernel(tc, h3, w4, b4, w5, b5, x, log_det_J, out_0,
 
         live = {}
 
-        w4_codes = keep.tile([P, PASSES, MID], U32, align_bytes=64)
-        w4_scales = keep.tile([P, PASSES, MID], U8, align_bytes=64)
+        w4_codes = keep.tile([P, PASSES, MID], U32, align_bytes=256)
+        w4_scales = keep.tile([P, PASSES, MID], U8, align_bytes=256)
         def regroup_w4(piece, g):
             w4_grouped = stage.tile([P, W4_PIECE, PACK], BF16, align_bytes=64)
             nc.vector.tensor_copy(
@@ -147,8 +147,8 @@ def tile_affinecoupling_pa_t_kernel(tc, h3, w4, b4, w5, b5, x, log_det_J, out_0,
                 in_=live["w4_grouped", piece, g][:].rearrange("p c t -> p (c t)"),
             )
 
-        w5_codes = keep.tile([P, PASSES, WIDTH], U32, align_bytes=64)
-        w5_scales = keep.tile([P, PASSES, WIDTH], U8, align_bytes=64)
+        w5_codes = keep.tile([P, PASSES, WIDTH], U32, align_bytes=256)
+        w5_scales = keep.tile([P, PASSES, WIDTH], U8, align_bytes=256)
 
         def pack_w5():
             w5_grouped = keep.tile([P, PASSES, WIDTH, PACK], BF16, align_bytes=64)
@@ -165,6 +165,8 @@ def tile_affinecoupling_pa_t_kernel(tc, h3, w4, b4, w5, b5, x, log_det_J, out_0,
 
         sums = keep.tile([P, TILES], F32)
         ALL = range(GROUP_TILES)
+        ROWS = slice(0, GROUP)
+        HALVES = (slice(0, GROUP // 2), slice(GROUP // 2, GROUP))
         PAIRS = (range(0, 2), range(2, GROUP_TILES))
 
         def vector_tiles(n):
@@ -194,61 +196,86 @@ def tile_affinecoupling_pa_t_kernel(tc, h3, w4, b4, w5, b5, x, log_det_J, out_0,
             for t in vector_tiles(n):
                 empty_xt(n, t, nc.vector.tensor_copy)
 
+        def h3_codes_of(n):
+            h3_codes = stage.tile([P, PASSES, GROUP], U32, align_bytes=256)
+            h3_scales = stage.tile([P, PASSES, GROUP], U8, align_bytes=256)
+            live["h3_codes", n] = h3_codes
+            live["h3_scales", n] = h3_scales
+            return h3_codes, h3_scales
+
+        def quantise_first_h3(rows):
+            for g in range(PASSES):
+                nc.vector.quantize_mx(
+                    out=live["h3_codes", 0][:, g, rows].bitcast(FP8X4),
+                    scales=live["h3_scales", 0][:, g, rows],
+                    in_=live["h3_grouped", 0][:, g, rows].rearrange("p b t -> p (b t)"),
+                )
+
         def quantise_h3(n):
-            h3_codes = stage.tile([P, PASSES, GROUP], U32, align_bytes=64)
-            h3_scales = stage.tile([P, PASSES, GROUP], U8, align_bytes=64)
+            h3_codes, h3_scales = h3_codes_of(n)
             nc.vector.quantize_mx(
                 out=h3_codes[:].rearrange("p g b -> p (g b)").bitcast(FP8X4),
                 scales=h3_scales[:].rearrange("p g b -> p (g b)"),
                 in_=live["h3_grouped", n][:].rearrange("p g b t -> p (g b t)"),
             )
-            live["h3_codes", n] = h3_codes
-            live["h3_scales", n] = h3_scales
 
-        def first_matmul(n, g2):
-            if g2 == 0:
+        def first_matmul(n, g2, rows=ROWS):
+            if g2 == 0 and rows.start == 0:
                 h4_planes = stage.tile([P, MID_TILES, GROUP], BF16)
                 live["h4_planes", n] = h4_planes
             for m in range(g2 * PACK, (g2 + 1) * PACK):
-                acc = psum.tile([P, GROUP], F32, tag="bank", bufs=BANKS)
+                acc = psum.tile([P, rows.stop - rows.start], F32, tag="bank", bufs=BANKS)
                 for g in range(PASSES):
                     nc.tensor.matmul_mx(
                         out=acc[:],
                         lhsT=w4_codes[:, g, m * P : (m + 1) * P].bitcast(FP8X4),
                         lhsT_scale=w4_scales[:, g, m * P : (m + 1) * P],
-                        rhs=live["h3_codes", n][:, g, :].bitcast(FP8X4),
-                        rhs_scale=live["h3_scales", n][:, g, :],
+                        rhs=live["h3_codes", n][:, g, rows].bitcast(FP8X4),
+                        rhs_scale=live["h3_scales", n][:, g, rows],
                         start=(g == 0),
                         stop=(g == PASSES - 1),
                     )
                 nc.scalar.activation(
-                    out=live["h4_planes", n][:, m, :],
+                    out=live["h4_planes", n][:, m, rows],
                     in_=acc[:],
                     func=ACT.Relu,
                     bias=b4_cols[:, m : m + 1],
                     scale=1.0,
                 )
 
-        def regroup_h4(n, g2):
-            h4_grouped = stage.tile([P, GROUP, PACK], BF16, align_bytes=64)
+        def regroup_h4(n, g2, rows=ROWS):
+            if g2 == 0 and rows.start == 0:
+                h4_grouped = stage.tile([P, PASSES, GROUP, PACK], BF16, align_bytes=64)
+                live["h4_grouped", n] = h4_grouped
             nc.vector.tensor_copy(
-                out=h4_grouped[:].rearrange("p (c i) j -> p c j i", i=4),
-                in_=live["h4_planes", n][:, g2 * PACK : (g2 + 1) * PACK, :].rearrange(
+                out=live["h4_grouped", n][:, g2, rows].rearrange("p (c i) j -> p c j i", i=4),
+                in_=live["h4_planes", n][:, g2 * PACK : (g2 + 1) * PACK, rows].rearrange(
                     "p j (c i) -> p c j i", i=4
                 ),
             )
-            live["h4_grouped", n, g2] = h4_grouped
 
-        def quantise_h4(n, g2):
-            if g2 == 0:
-                h4_codes = stage.tile([P, PASSES, GROUP], U32, align_bytes=64)
-                h4_scales = stage.tile([P, PASSES, GROUP], U8, align_bytes=64)
+        def h4_codes_of(n):
+            if ("h4_codes", n) not in live:
+                h4_codes = stage.tile([P, PASSES, GROUP], U32, align_bytes=256)
+                h4_scales = stage.tile([P, PASSES, GROUP], U8, align_bytes=256)
                 live["h4_codes", n] = h4_codes
                 live["h4_scales", n] = h4_scales
+            return live["h4_codes", n], live["h4_scales", n]
+
+        def quantise_h4(n):
+            h4_codes, h4_scales = h4_codes_of(n)
             nc.vector.quantize_mx(
-                out=live["h4_codes", n][:, g2, :].bitcast(FP8X4),
-                scales=live["h4_scales", n][:, g2, :],
-                in_=live["h4_grouped", n, g2][:].rearrange("p b j -> p (b j)"),
+                out=h4_codes[:].rearrange("p g b -> p (g b)").bitcast(FP8X4),
+                scales=h4_scales[:].rearrange("p g b -> p (g b)"),
+                in_=live["h4_grouped", n][:].rearrange("p g b j -> p (g b j)"),
+            )
+
+        def quantise_h4_part(n, g2, rows=ROWS):
+            h4_codes, h4_scales = h4_codes_of(n)
+            nc.vector.quantize_mx(
+                out=h4_codes[:, g2, rows].bitcast(FP8X4),
+                scales=h4_scales[:, g2, rows],
+                in_=live["h4_grouped", n][:, g2, rows].rearrange("p b j -> p (b j)"),
             )
 
         def second_matmul(n):
@@ -308,7 +335,7 @@ def tile_affinecoupling_pa_t_kernel(tc, h3, w4, b4, w5, b5, x, log_det_J, out_0,
             )
 
         def pass_x(n):
-            y_planes = stage.tile([P, GROUP_TILES, 2, HALF], F32)
+            y_planes = stage.tile([P, GROUP_TILES, 2, HALF], F32, bufs=3)
             live["y_planes", n] = y_planes
             nc.gpsimd.tensor_scalar(
                 out=y_planes[:, :, 0, :],
@@ -333,7 +360,7 @@ def tile_affinecoupling_pa_t_kernel(tc, h3, w4, b4, w5, b5, x, log_det_J, out_0,
 
         def store_y(n, tiles, interleave):
             if tiles.start == 0:
-                y = stage.tile([P, GROUP_TILES, HALF, 2], F32)
+                y = stage.tile([P, GROUP_TILES, HALF, 2], F32, bufs=3)
                 live["y", n] = y
             y = live["y", n]
             interleave(out=part(y, tiles), in_=part(live["y_planes", n], tiles).rearrange("p t e c -> p t c e"))
@@ -347,21 +374,19 @@ def tile_affinecoupling_pa_t_kernel(tc, h3, w4, b4, w5, b5, x, log_det_J, out_0,
             return 0 <= k < GROUPS
 
         def one_round(n):
-            first_matmul(n, 0)
-            if n == 0:
-                transpose_h3(1)
+            if n > 0:
+                first_matmul(n, 0)
             first_matmul(n, 1)
-            if n == 0:
-                empty_vector_tiles(1)
-                pack_w5()
             if on(n - 1):
                 regroup_h4(n - 1, 1)
             if on(n - 3):
                 scale_x(n - 3, ALL)
             if on(n - 1):
-                quantise_h4(n - 1, 1)
+                quantise_h4(n - 1)
             quantise_h3(n + 1)
             regroup_h4(n, 0)
+            if n == 0:
+                pack_w5()
             if on(n - 1):
                 second_matmul(n - 1)
             if on(n - 2):
@@ -377,37 +402,39 @@ def tile_affinecoupling_pa_t_kernel(tc, h3, w4, b4, w5, b5, x, log_det_J, out_0,
                     add_b5(n - 1, pair)
             if on(n + 2):
                 empty_vector_tiles(n + 2)
-            quantise_h4(n, 0)
 
         def last_rounds():
             n = GROUPS - 1
             first_matmul(n, 0)
             regroup_h4(n - 1, 1)
             scale_x(n - 3, ALL)
-            quantise_h4(n - 1, 1)
-            first_matmul(n, 1)
+            quantise_h4(n - 1)
+            for rows in HALVES:
+                first_matmul(n, 1, rows)
             second_matmul(n - 1)
             log_scale(n - 2, ALL)
             regroup_h4(n, 0)
             shift_x(n - 3, ALL)
             store_y(n - 3, ALL, interleave_on_gpsimd)
             pass_x(n - 2)
-            quantise_h4(n, 0)
-            regroup_h4(n, 1)
+            quantise_h4_part(n, 0)
+            regroup_h4(n, 1, HALVES[0])
             add_b5(n - 1, PAIRS[0])
-            quantise_h4(n, 1)
-            second_matmul(n)
+            quantise_h4_part(n, 1, HALVES[0])
+            regroup_h4(n, 1, HALVES[1])
             add_b5(n - 1, PAIRS[1])
+            quantise_h4_part(n, 1, HALVES[1])
+            second_matmul(n)
             log_scale(n - 1, ALL)
             scale_x(n - 2, ALL)
             pass_x(n - 1)
             shift_x(n - 2, ALL)
+            add_b5(n, PAIRS[0])
+            log_scale(n, PAIRS[0])
             store_y(n - 2, ALL, nc.scalar.copy)
-            for pair in PAIRS:
-                add_b5(n, pair)
-            for pair in PAIRS:
-                log_scale(n, pair)
             scale_x(n - 1, ALL)
+            add_b5(n, PAIRS[1])
+            log_scale(n, PAIRS[1])
             shift_x(n - 1, ALL)
             pass_x(n)
             scale_x(n, PAIRS[0])
@@ -416,6 +443,9 @@ def tile_affinecoupling_pa_t_kernel(tc, h3, w4, b4, w5, b5, x, log_det_J, out_0,
             scale_x(n, PAIRS[1])
             store_y(n, PAIRS[0], nc.vector.tensor_copy)
             shift_x(n, PAIRS[1])
+            log_det = keep.tile([P, TILES], F32)
+            nc.vector.tensor_tensor(out=log_det[:], in0=sums[:], in1=ldj[:], op=ALU.add)
+            nc.sync.dma_start(out=out_1.rearrange("(p t) -> p t", t=TILES), in_=log_det[:])
             store_y(n, PAIRS[1], nc.vector.tensor_copy)
 
         pass_x(0)
@@ -425,19 +455,19 @@ def tile_affinecoupling_pa_t_kernel(tc, h3, w4, b4, w5, b5, x, log_det_J, out_0,
         quantise_w4(0, 0)
         quantise_w4(0, 1)
         transpose_h3(0)
-        empty_vector_tiles(0)
         spread_biases()
-        warm_up(4)
-        quantise_h3(0)
+        h3_codes_of(0)
+        quantise_first_h3(HALVES[0])
         keep_biases()
+        first_matmul(0, 0, HALVES[0])
+        quantise_first_h3(HALVES[1])
+        first_matmul(0, 0, HALVES[1])
+        transpose_h3(1)
         regroup_w4(1, 0)
         regroup_w4(1, 1)
         quantise_w4(1, 0)
         quantise_w4(1, 1)
+        empty_vector_tiles(1)
         for n in range(GROUPS - 1):
             one_round(n)
         last_rounds()
-
-        log_det = keep.tile([P, TILES], F32)
-        nc.vector.tensor_tensor(out=log_det[:], in0=sums[:], in1=ldj[:], op=ALU.add)
-        nc.sync.dma_start(out=out_1.rearrange("(p t) -> p t", t=TILES), in_=log_det[:])

@@ -26,6 +26,8 @@ GROUPS = TILES // GROUP_TILES
 W4_PIECE = 512
 BANKS = 8
 
+HALVES = (slice(0, 256), slice(256, 512))
+
 FLOPS = 2 * BATCH * MID * MID + 2 * BATCH * MID * WIDTH
 
 
@@ -34,7 +36,7 @@ def tile_affinecoupling_pa_t_kernel(tc, h3, w4, b4, w5, b5, x, log_det_J, out_0,
     with ExitStack() as ctx:
         ctx.enter_context(tc.manual_schedule())
         keep = ctx.enter_context(tc.tile_pool(name="keep", bufs=1))
-        h3_pool = ctx.enter_context(tc.tile_pool(name="h3_pool", bufs=GROUPS - 2))
+        h3_pool = ctx.enter_context(tc.tile_pool(name="h3_pool", bufs=GROUPS - 3))
         stage = ctx.enter_context(tc.tile_pool(name="stage", bufs=2))
         psum = ctx.enter_context(tc.psum_pool(name="psum", bufs=2))
 
@@ -166,7 +168,6 @@ def tile_affinecoupling_pa_t_kernel(tc, h3, w4, b4, w5, b5, x, log_det_J, out_0,
         sums = keep.tile([P, TILES], F32)
         ALL = range(GROUP_TILES)
         ROWS = slice(0, GROUP)
-        HALVES = (slice(0, GROUP // 2), slice(GROUP // 2, GROUP))
         PAIRS = (range(0, 2), range(2, GROUP_TILES))
 
         def vector_tiles(n):
@@ -294,7 +295,7 @@ def tile_affinecoupling_pa_t_kernel(tc, h3, w4, b4, w5, b5, x, log_det_J, out_0,
                             stop=(g == PASSES - 1),
                         )
                 live["v", n, pair] = v
-            planes = stage.tile([P, GROUP_TILES, 2, HALF], F32)
+            planes = stage.tile([P, GROUP_TILES, 2, HALF], F32, bufs=3)
             ls = stage.tile([P, GROUP_TILES, HALF], F32)
             scale = stage.tile([P, GROUP_TILES, HALF], F32)
             scaled = stage.tile([P, GROUP_TILES, HALF], F32)
@@ -326,6 +327,9 @@ def tile_affinecoupling_pa_t_kernel(tc, h3, w4, b4, w5, b5, x, log_det_J, out_0,
                     func=ACT.Tanh,
                     accum_out=sums[:, tile_index : tile_index + 1],
                 )
+
+        def exponentiate(n, tiles):
+            planes, ls, scale, scaled = live["coupling", n]
             nc.scalar.activation(out=part(scale, tiles), in_=part(ls, tiles), func=ACT.Exp)
 
         def scale_x(n, tiles):
@@ -334,17 +338,10 @@ def tile_affinecoupling_pa_t_kernel(tc, h3, w4, b4, w5, b5, x, log_det_J, out_0,
                 out=part(scaled, tiles), in0=x_pairs(n, tiles)[:, :, :, 1], in1=part(scale, tiles), op=ALU.mult
             )
 
-        def pass_x(n):
+        def pass_x(n, copy):
             y_planes = stage.tile([P, GROUP_TILES, 2, HALF], F32, bufs=3)
             live["y_planes", n] = y_planes
-            nc.gpsimd.tensor_scalar(
-                out=y_planes[:, :, 0, :],
-                in0=x_pairs(n, ALL)[:, :, :, 0],
-                scalar1=1.0,
-                scalar2=0.0,
-                op0=ALU.mult,
-                op1=ALU.add,
-            )
+            copy(out=y_planes[:, :, 0, :], in_=x_pairs(n, ALL)[:, :, :, 0])
 
         def shift_x(n, tiles):
             planes, ls, scale, scaled = live["coupling", n]
@@ -355,7 +352,7 @@ def tile_affinecoupling_pa_t_kernel(tc, h3, w4, b4, w5, b5, x, log_det_J, out_0,
                 op=ALU.add,
             )
 
-        def interleave_on_gpsimd(out, in_):
+        def copy_on_gpsimd(out, in_):
             nc.gpsimd.tensor_scalar(out=out, in0=in_, scalar1=1.0, scalar2=0.0, op0=ALU.mult, op1=ALU.add)
 
         def store_y(n, tiles, interleave):
@@ -384,6 +381,8 @@ def tile_affinecoupling_pa_t_kernel(tc, h3, w4, b4, w5, b5, x, log_det_J, out_0,
             if on(n - 1):
                 quantise_h4(n - 1)
             quantise_h3(n + 1)
+            if on(n - 3):
+                shift_x(n - 3, ALL)
             regroup_h4(n, 0)
             if n == 0:
                 pack_w5()
@@ -391,12 +390,12 @@ def tile_affinecoupling_pa_t_kernel(tc, h3, w4, b4, w5, b5, x, log_det_J, out_0,
                 second_matmul(n - 1)
             if on(n - 2):
                 log_scale(n - 2, ALL)
+                exponentiate(n - 2, ALL)
             if on(n + 2):
                 transpose_h3(n + 2)
             if on(n - 3):
-                shift_x(n - 3, ALL)
-                store_y(n - 3, ALL, interleave_on_gpsimd)
-                pass_x(n - 2)
+                store_y(n - 3, ALL, copy_on_gpsimd)
+                pass_x(n - 2, copy_on_gpsimd)
             if on(n - 1):
                 for pair in PAIRS:
                     add_b5(n - 1, pair)
@@ -413,10 +412,11 @@ def tile_affinecoupling_pa_t_kernel(tc, h3, w4, b4, w5, b5, x, log_det_J, out_0,
                 first_matmul(n, 1, rows)
             second_matmul(n - 1)
             log_scale(n - 2, ALL)
+            pass_x(n - 2, nc.scalar.copy)
+            exponentiate(n - 2, ALL)
             regroup_h4(n, 0)
             shift_x(n - 3, ALL)
-            store_y(n - 3, ALL, interleave_on_gpsimd)
-            pass_x(n - 2)
+            store_y(n - 3, ALL, nc.scalar.copy)
             quantise_h4_part(n, 0)
             regroup_h4(n, 1, HALVES[0])
             add_b5(n - 1, PAIRS[0])
@@ -425,18 +425,22 @@ def tile_affinecoupling_pa_t_kernel(tc, h3, w4, b4, w5, b5, x, log_det_J, out_0,
             add_b5(n - 1, PAIRS[1])
             quantise_h4_part(n, 1, HALVES[1])
             second_matmul(n)
-            log_scale(n - 1, ALL)
+            log_scale(n - 1, PAIRS[0])
+            pass_x(n - 1, nc.scalar.copy)
+            log_scale(n - 1, PAIRS[1])
+            exponentiate(n - 1, ALL)
             scale_x(n - 2, ALL)
-            pass_x(n - 1)
-            shift_x(n - 2, ALL)
             add_b5(n, PAIRS[0])
+            shift_x(n - 2, ALL)
             log_scale(n, PAIRS[0])
+            exponentiate(n, PAIRS[0])
             store_y(n - 2, ALL, nc.scalar.copy)
+            pass_x(n, nc.scalar.copy)
             scale_x(n - 1, ALL)
             add_b5(n, PAIRS[1])
             log_scale(n, PAIRS[1])
+            exponentiate(n, PAIRS[1])
             shift_x(n - 1, ALL)
-            pass_x(n)
             scale_x(n, PAIRS[0])
             store_y(n - 1, ALL, nc.vector.tensor_copy)
             shift_x(n, PAIRS[0])
@@ -448,7 +452,7 @@ def tile_affinecoupling_pa_t_kernel(tc, h3, w4, b4, w5, b5, x, log_det_J, out_0,
             nc.sync.dma_start(out=out_1.rearrange("(p t) -> p t", t=TILES), in_=log_det[:])
             store_y(n, PAIRS[1], nc.vector.tensor_copy)
 
-        pass_x(0)
+        pass_x(0, copy_on_gpsimd)
         warm_up(6)
         regroup_w4(0, 0)
         regroup_w4(0, 1)

@@ -65,10 +65,12 @@ def tile_affinecoupling_pa_t_kernel(tc, h3, w4, b4, w5, b5, x, log_det_J, out_0,
             for t in range(GROUP_TILES):
                 nc.sync.dma_start(out=h3_raw[n][:, t, :], in_=h3_rows[:, n * GROUP_TILES + t, :])
 
-        bias_rows = keep.tile([P, MID + WIDTH], BF16)
-        nc.gpsimd.memset(bias_rows[:], 0.0)
-        nc.scalar.dma_start(out=bias_rows[0:1, 0:MID], in_=b4.rearrange("(o k) -> o k", o=1))
-        nc.scalar.dma_start(out=bias_rows[0:1, MID : MID + WIDTH], in_=b5.rearrange("(o k) -> o k", o=1))
+        b4_cols = keep.tile([P, PASSES, PACK], BF16)
+        nc.scalar.dma_start(out=b4_cols[:], in_=b4.rearrange("(g p j) -> p g j", p=P, j=PACK))
+
+        b5_row = keep.tile([P, WIDTH], BF16)
+        nc.gpsimd.memset(b5_row[:], 0.0)
+        nc.scalar.dma_start(out=b5_row[0:1, :], in_=b5.rearrange("(o k) -> o k", o=1))
 
         w5_raw = keep.tile([P, PASSES, PACK, WIDTH], BF16)
         x_all = keep.tile([P, TILES, WIDTH], BF16)
@@ -93,33 +95,18 @@ def tile_affinecoupling_pa_t_kernel(tc, h3, w4, b4, w5, b5, x, log_det_J, out_0,
 
         ones = keep.tile([P, P], BF16)
         nc.vector.memset(ones[:], 1.0)
-        b4_cols = keep.tile([P, MID_TILES], F32)
         b5_planes = keep.tile([P, 2, HALF], F32)
 
-        def spread_biases():
-            spread = psum.tile([P, WIDTH + MID_TILES], F32, tag="bank", bufs=BANKS)
+        def spread_b5():
+            spread = psum.tile([P, WIDTH], F32, tag="bank", bufs=BANKS)
             nc.tensor.matmul(
-                spread[:, 0:WIDTH],
+                spread[:],
                 lhsT=ones[:],
-                rhs=bias_rows[:, MID : MID + WIDTH].rearrange("p (c e) -> p e c", e=2),
+                rhs=b5_row[:].rearrange("p (c e) -> p e c", e=2),
                 start=True,
                 stop=True,
             )
-            for m in range(MID_TILES):
-                g, j = divmod(m, PACK)
-                nc.tensor.matmul(
-                    spread[:, WIDTH + m : WIDTH + m + 1],
-                    lhsT=bias_rows[:, g * K_PASS + j : (g + 1) * K_PASS : PACK],
-                    rhs=ones[:, 0:1],
-                    start=True,
-                    stop=True,
-                )
-            live["spread"] = spread
-
-        def keep_biases():
-            spread = live["spread"]
-            nc.vector.tensor_copy(out=b4_cols[:], in_=spread[:, WIDTH : WIDTH + MID_TILES])
-            nc.vector.tensor_copy(out=b5_planes[:].rearrange("p e c -> p (e c)"), in_=spread[:, 0:WIDTH])
+            nc.scalar.copy(out=b5_planes[:].rearrange("p e c -> p (e c)"), in_=spread[:])
 
         zeros = keep.tile([P, GROUP], BF16)
         nc.vector.memset(zeros[:], 0.0)
@@ -240,7 +227,7 @@ def tile_affinecoupling_pa_t_kernel(tc, h3, w4, b4, w5, b5, x, log_det_J, out_0,
                     out=live["h4_planes", n][:, m, rows],
                     in_=acc[:],
                     func=ACT.Relu,
-                    bias=b4_cols[:, m : m + 1],
+                    bias=b4_cols[:, g2, m % PACK : m % PACK + 1],
                     scale=1.0,
                 )
 
@@ -459,14 +446,13 @@ def tile_affinecoupling_pa_t_kernel(tc, h3, w4, b4, w5, b5, x, log_det_J, out_0,
         quantise_w4(0, 0)
         quantise_w4(0, 1)
         transpose_h3(0)
-        spread_biases()
         h3_codes_of(0)
         quantise_first_h3(HALVES[0])
-        keep_biases()
         first_matmul(0, 0, HALVES[0])
         quantise_first_h3(HALVES[1])
         first_matmul(0, 0, HALVES[1])
         transpose_h3(1)
+        spread_b5()
         regroup_w4(1, 0)
         regroup_w4(1, 1)
         quantise_w4(1, 0)

@@ -24,6 +24,8 @@ GROUP_TILES = 4
 GROUP = GROUP_TILES * P
 GROUPS = TILES // GROUP_TILES
 W4_PIECE = 512
+SORTED_GROUPS = range(3, 6)
+SORTED_TILES = 2
 BANKS = 8
 
 HALVES = (slice(0, 256), slice(256, 512))
@@ -81,9 +83,10 @@ def tile_affinecoupling_pa_t_kernel(tc, h3, w4, b4, w5, b5, x, log_det_J, out_0,
         load_h3(1)
         nc.sync.dma_start(out=w5_raw[:], in_=w5.rearrange("(g p j) n -> p g j n", j=PACK, p=P))
         load_h3(2)
-        nc.sync.dma_start(out=x_all[:], in_=x_rows)
         for n in range(3, GROUPS):
             load_h3(n)
+            if n == 4:
+                nc.sync.dma_start(out=x_all[:], in_=x_rows)
         nc.sync.dma_start(out=ldj[:], in_=log_det_J.rearrange("(p t) -> p t", t=TILES))
 
         warm = keep.tile([P, 1], F32)
@@ -160,16 +163,27 @@ def tile_affinecoupling_pa_t_kernel(tc, h3, w4, b4, w5, b5, x, log_det_J, out_0,
         def vector_tiles(n):
             return range(n % 2)
 
+        def sort_words(n, copy):
+            h3_words = stage.tile([P, SORTED_TILES, PASSES * 2, P], F32)
+            live["h3_words", n] = h3_words
+            copy(
+                out=h3_words[:].rearrange("p t (g u) w -> p (t g) u w", u=2),
+                in_=h3_raw[n][:, 0:SORTED_TILES].bitcast(F32).rearrange("p t (g w u) -> p (t g) u w", g=PASSES, u=2),
+            )
+
+        def words_of(n, t, block):
+            if n in SORTED_GROUPS and t < SORTED_TILES:
+                return live["h3_words", n][:, t, block, :]
+            g, u = divmod(block, 2)
+            return h3_raw[n][:].bitcast(F32)[:, t, g * 2 * P + u : (g + 1) * 2 * P : 2]
+
         def transpose_h3(n):
             h3_grouped = stage.tile([P, PASSES, GROUP, PACK], BF16, align_bytes=64, bufs=3)
             live["h3_grouped", n] = h3_grouped
-            raw_words = h3_raw[n][:].bitcast(F32)
             for t in range(GROUP_TILES):
                 xt = psum.tile([P, PASSES * 2, P], F32, tag="bank", bufs=BANKS)
                 for block in range(PASSES * 2):
-                    g, u = divmod(block, 2)
-                    words = slice(g * 2 * P + u, (g + 1) * 2 * P, 2)
-                    nc.tensor.transpose(xt[:, block, :], raw_words[:, t, words], ident_f32[:])
+                    nc.tensor.transpose(xt[:, block, :], words_of(n, t, block), ident_f32[:])
                 live["xt", n, t] = xt
                 if t not in vector_tiles(n):
                     empty_xt(n, t, nc.scalar.copy)
@@ -373,6 +387,8 @@ def tile_affinecoupling_pa_t_kernel(tc, h3, w4, b4, w5, b5, x, log_det_J, out_0,
             regroup_h4(n, 0)
             if n == 0:
                 pack_w5()
+            if n + 3 in SORTED_GROUPS and n == 1:
+                sort_words(n + 3, nc.scalar.copy)
             if on(n - 1):
                 second_matmul(n - 1)
             if on(n - 2):
@@ -388,6 +404,8 @@ def tile_affinecoupling_pa_t_kernel(tc, h3, w4, b4, w5, b5, x, log_det_J, out_0,
                     add_b5(n - 1, pair)
             if on(n + 2):
                 empty_vector_tiles(n + 2)
+            if n + 3 in SORTED_GROUPS and n != 1:
+                sort_words(n + 3, nc.vector.tensor_copy)
 
         def last_rounds():
             n = GROUPS - 1

from contextlib import ExitStack

import concourse.mybir as mybir
from concourse.masks import make_identity

BF16 = mybir.dt.bfloat16
F32 = mybir.dt.float32
U32 = mybir.dt.uint32
U8 = mybir.dt.uint8
FP8X4 = mybir.dt.float8_e4m3fn_x4
ACT = mybir.ActivationFunctionType
ALU = mybir.AluOpType

P = 128
PACK = 4
K_PASS = P * PACK

BATCH, MID, WIDTH = 4096, 1024, 256
HALF = WIDTH // 2
PASSES = MID // K_PASS
MID_TILES = MID // P
TILES = BATCH // P
GROUP_TILES = 4
GROUP = GROUP_TILES * P
GROUPS = TILES // GROUP_TILES
W4_PIECE = 512
SORTED_GROUPS = range(3, 6)
SORTED_TILES = 2
BANKS = 8

HALVES = (slice(0, 256), slice(256, 512))

FLOPS = 2 * BATCH * MID * MID + 2 * BATCH * MID * WIDTH


def tile_affinecoupling_pa_t_kernel(tc, h3, w4, b4, w5, b5, x, log_det_J, out_0, out_1):
    nc = tc.nc
    with ExitStack() as ctx:
        ctx.enter_context(tc.manual_schedule())
        keep = ctx.enter_context(tc.tile_pool(name="keep", bufs=1))
        h3_pool = ctx.enter_context(tc.tile_pool(name="h3_pool", bufs=GROUPS - 3))
        stage = ctx.enter_context(tc.tile_pool(name="stage", bufs=2))
        psum = ctx.enter_context(tc.psum_pool(name="psum", bufs=2))

        h3_rows = h3.rearrange("(p t) k -> p t k", t=TILES)
        x_rows = x.rearrange("(p t) c -> p t c", t=TILES)
        y_rows = out_0.rearrange("(p t) c -> p t c", t=TILES)

        w4_raw = []
        for piece in range(MID // W4_PIECE):
            w4_piece = keep.tile([P, PASSES, PACK, W4_PIECE], BF16, name="w4_raw", bufs=MID // W4_PIECE)
            w4_raw.append(w4_piece)
        h3_raw = []
        for n in range(GROUPS):
            raw = h3_pool.tile([P, GROUP_TILES, MID], BF16, name="h3_raw")
            h3_raw.append(raw)

        def load_w4(piece):
            cols = slice(piece * W4_PIECE, (piece + 1) * W4_PIECE)
            for g in range(PASSES):
                nc.sync.dma_start(
                    out=w4_raw[piece][:, g],
                    in_=w4[g * K_PASS : (g + 1) * K_PASS, cols].rearrange("(q j) c -> q j c", j=PACK),
                )

        def load_h3(n):
            for t in range(GROUP_TILES):
                nc.sync.dma_start(out=h3_raw[n][:, t, :], in_=h3_rows[:, n * GROUP_TILES + t, :])

        b4_cols = keep.tile([P, PASSES, PACK], BF16)
        nc.scalar.dma_start(out=b4_cols[:], in_=b4.rearrange("(g p j) -> p g j", p=P, j=PACK))

        b5_row = keep.tile([P, WIDTH], BF16)
        nc.gpsimd.memset(b5_row[:], 0.0)
        nc.scalar.dma_start(out=b5_row[0:1, :], in_=b5.rearrange("(o k) -> o k", o=1))

        w5_raw = keep.tile([P, PASSES, PACK, WIDTH], BF16)
        x_all = keep.tile([P, TILES, WIDTH], BF16)
        ldj = keep.tile([P, TILES], BF16)
        load_w4(0)
        load_h3(0)
        load_w4(1)
        load_h3(1)
        nc.sync.dma_start(out=w5_raw[:], in_=w5.rearrange("(g p j) n -> p g j n", j=PACK, p=P))
        load_h3(2)
        for n in range(3, GROUPS):
            load_h3(n)
            if n == 4:
                nc.sync.dma_start(out=x_all[:], in_=x_rows)
        nc.sync.dma_start(out=ldj[:], in_=log_det_J.rearrange("(p t) -> p t", t=TILES))

        warm = keep.tile([P, 1], F32)
        nc.vector.memset(warm[:], 0.0)
        nc.scalar.activation(out=warm[:], in_=warm[:], func=ACT.Tanh)

        ident_f32 = keep.tile([P, P], F32)
        make_identity(nc, ident_f32[:])

        ones = keep.tile([P, P], BF16)
        nc.vector.memset(ones[:], 1.0)
        b5_planes = keep.tile([P, 2, HALF], F32)

        def spread_b5():
            spread = psum.tile([P, WIDTH], F32, tag="bank", bufs=BANKS)
            nc.tensor.matmul(
                spread[:],
                lhsT=ones[:],
                rhs=b5_row[:].rearrange("p (c e) -> p e c", e=2),
                start=True,
                stop=True,
            )
            nc.scalar.copy(out=b5_planes[:].rearrange("p e c -> p (e c)"), in_=spread[:])

        zeros = keep.tile([P, GROUP], BF16)
        nc.vector.memset(zeros[:], 0.0)

        def warm_up(matmuls):
            idle = psum.tile([P, GROUP], F32, tag="bank", bufs=BANKS)
            for i in range(matmuls):
                nc.tensor.matmul(idle[:], lhsT=zeros[:, 0:P], rhs=zeros[:], start=True, stop=True)

        live = {}

        w4_codes = keep.tile([P, PASSES, MID], U32, align_bytes=256)
        w4_scales = keep.tile([P, PASSES, MID], U8, align_bytes=256)
        def regroup_w4(piece, g):
            w4_grouped = stage.tile([P, W4_PIECE, PACK], BF16, align_bytes=64)
            nc.vector.tensor_copy(
                out=w4_grouped[:].rearrange("p (t m) j -> p t m j", t=PACK),
                in_=w4_raw[piece][:, g].rearrange("p j (m t) -> p t m j", t=PACK),
            )
            live["w4_grouped", piece, g] = w4_grouped

        def quantise_w4(piece, g):
            cols = slice(piece * W4_PIECE, (piece + 1) * W4_PIECE)
            nc.vector.quantize_mx(
                out=w4_codes[:, g, cols].bitcast(FP8X4),
                scales=w4_scales[:, g, cols],
                in_=live["w4_grouped", piece, g][:].rearrange("p c t -> p (c t)"),
            )

        w5_codes = keep.tile([P, PASSES, WIDTH], U32, align_bytes=256)
        w5_scales = keep.tile([P, PASSES, WIDTH], U8, align_bytes=256)

        def pack_w5():
            w5_grouped = keep.tile([P, PASSES, WIDTH, PACK], BF16, align_bytes=64)
            for g in range(PASSES):
                nc.vector.tensor_copy(
                    out=w5_grouped[:, g].rearrange("p (e c) j -> p e c j", e=2),
                    in_=w5_raw[:, g].rearrange("p j (c e) -> p e c j", e=2),
                )
            nc.vector.quantize_mx(
                out=w5_codes[:].rearrange("p g n -> p (g n)").bitcast(FP8X4),
                scales=w5_scales[:].rearrange("p g n -> p (g n)"),
                in_=w5_grouped[:].rearrange("p g n j -> p (g n j)"),
            )

        sums = keep.tile([P, TILES], F32)
        ALL = range(GROUP_TILES)
        ROWS = slice(0, GROUP)
        PAIRS = (range(0, 2), range(2, GROUP_TILES))

        def vector_tiles(n):
            return range(n % 2)

        def sort_words(n, copy):
            h3_words = stage.tile([P, SORTED_TILES, PASSES * 2, P], F32)
            live["h3_words", n] = h3_words
            copy(
                out=h3_words[:].rearrange("p t (g u) w -> p (t g) u w", u=2),
                in_=h3_raw[n][:, 0:SORTED_TILES].bitcast(F32).rearrange("p t (g w u) -> p (t g) u w", g=PASSES, u=2),
            )

        def words_of(n, t, block):
            if n in SORTED_GROUPS and t < SORTED_TILES:
                return live["h3_words", n][:, t, block, :]
            g, u = divmod(block, 2)
            return h3_raw[n][:].bitcast(F32)[:, t, g * 2 * P + u : (g + 1) * 2 * P : 2]

        def transpose_h3(n):
            h3_grouped = stage.tile([P, PASSES, GROUP, PACK], BF16, align_bytes=64, bufs=3)
            live["h3_grouped", n] = h3_grouped
            for t in range(GROUP_TILES):
                xt = psum.tile([P, PASSES * 2, P], F32, tag="bank", bufs=BANKS)
                for block in range(PASSES * 2):
                    nc.tensor.transpose(xt[:, block, :], words_of(n, t, block), ident_f32[:])
                live["xt", n, t] = xt
                if t not in vector_tiles(n):
                    empty_xt(n, t, nc.scalar.copy)

        def empty_xt(n, t, copy):
            copy(
                out=live["h3_grouped", n][:].bitcast(F32)[:, :, t * P : (t + 1) * P, :],
                in_=live["xt", n, t][:].rearrange("p (g u) r -> p g r u", u=2),
            )

        def empty_vector_tiles(n):
            for t in vector_tiles(n):
                empty_xt(n, t, nc.vector.tensor_copy)

        def h3_codes_of(n):
            h3_codes = stage.tile([P, PASSES, GROUP], U32, align_bytes=256)
            h3_scales = stage.tile([P, PASSES, GROUP], U8, align_bytes=256)
            live["h3_codes", n] = h3_codes
            live["h3_scales", n] = h3_scales
            return h3_codes, h3_scales

        def quantise_first_h3(rows):
            for g in range(PASSES):
                nc.vector.quantize_mx(
                    out=live["h3_codes", 0][:, g, rows].bitcast(FP8X4),
                    scales=live["h3_scales", 0][:, g, rows],
                    in_=live["h3_grouped", 0][:, g, rows].rearrange("p b t -> p (b t)"),
                )

        def quantise_h3(n):
            h3_codes, h3_scales = h3_codes_of(n)
            nc.vector.quantize_mx(
                out=h3_codes[:].rearrange("p g b -> p (g b)").bitcast(FP8X4),
                scales=h3_scales[:].rearrange("p g b -> p (g b)"),
                in_=live["h3_grouped", n][:].rearrange("p g b t -> p (g b t)"),
            )

        def first_matmul(n, g2, rows=ROWS):
            if g2 == 0 and rows.start == 0:
                h4_planes = stage.tile([P, MID_TILES, GROUP], BF16)
                live["h4_planes", n] = h4_planes
            for m in range(g2 * PACK, (g2 + 1) * PACK):
                acc = psum.tile([P, rows.stop - rows.start], F32, tag="bank", bufs=BANKS)
                for g in range(PASSES):
                    nc.tensor.matmul_mx(
                        out=acc[:],
                        lhsT=w4_codes[:, g, m * P : (m + 1) * P].bitcast(FP8X4),
                        lhsT_scale=w4_scales[:, g, m * P : (m + 1) * P],
                        rhs=live["h3_codes", n][:, g, rows].bitcast(FP8X4),
                        rhs_scale=live["h3_scales", n][:, g, rows],
                        start=(g == 0),
                        stop=(g == PASSES - 1),
                    )
                nc.scalar.activation(
                    out=live["h4_planes", n][:, m, rows],
                    in_=acc[:],
                    func=ACT.Relu,
                    bias=b4_cols[:, g2, m % PACK : m % PACK + 1],
                    scale=1.0,
                )

        def regroup_h4(n, g2, rows=ROWS):
            if g2 == 0 and rows.start == 0:
                h4_grouped = stage.tile([P, PASSES, GROUP, PACK], BF16, align_bytes=64)
                live["h4_grouped", n] = h4_grouped
            nc.vector.tensor_copy(
                out=live["h4_grouped", n][:, g2, rows].rearrange("p (c i) j -> p c j i", i=4),
                in_=live["h4_planes", n][:, g2 * PACK : (g2 + 1) * PACK, rows].rearrange(
                    "p j (c i) -> p c j i", i=4
                ),
            )

        def h4_codes_of(n):
            if ("h4_codes", n) not in live:
                h4_codes = stage.tile([P, PASSES, GROUP], U32, align_bytes=256)
                h4_scales = stage.tile([P, PASSES, GROUP], U8, align_bytes=256)
                live["h4_codes", n] = h4_codes
                live["h4_scales", n] = h4_scales
            return live["h4_codes", n], live["h4_scales", n]

        def quantise_h4(n):
            h4_codes, h4_scales = h4_codes_of(n)
            nc.vector.quantize_mx(
                out=h4_codes[:].rearrange("p g b -> p (g b)").bitcast(FP8X4),
                scales=h4_scales[:].rearrange("p g b -> p (g b)"),
                in_=live["h4_grouped", n][:].rearrange("p g b j -> p (g b j)"),
            )

        def quantise_h4_part(n, g2, rows=ROWS):
            h4_codes, h4_scales = h4_codes_of(n)
            nc.vector.quantize_mx(
                out=h4_codes[:, g2, rows].bitcast(FP8X4),
                scales=h4_scales[:, g2, rows],
                in_=live["h4_grouped", n][:, g2, rows].rearrange("p b j -> p (b j)"),
            )

        def second_matmul(n):
            for pair in PAIRS:
                v = psum.tile([P, 2, WIDTH], F32, tag="bank", bufs=BANKS)
                for i, t in enumerate(pair):
                    rows = slice(t * P, (t + 1) * P)
                    for g in range(PASSES):
                        nc.tensor.matmul_mx(
                            out=v[:, i, :],
                            lhsT=live["h4_codes", n][:, g, rows].bitcast(FP8X4),
                            lhsT_scale=live["h4_scales", n][:, g, rows],
                            rhs=w5_codes[:, g, :].bitcast(FP8X4),
                            rhs_scale=w5_scales[:, g, :],
                            start=(g == 0),
                            stop=(g == PASSES - 1),
                        )
                live["v", n, pair] = v
            planes = stage.tile([P, GROUP_TILES, 2, HALF], F32, bufs=3)
            ls = stage.tile([P, GROUP_TILES, HALF], F32)
            scale = stage.tile([P, GROUP_TILES, HALF], F32)
            scaled = stage.tile([P, GROUP_TILES, HALF], F32)
            live["coupling", n] = planes, ls, scale, scaled

        def part(tile, tiles):
            return tile[:, tiles.start : tiles.stop]

        def x_pairs(n, tiles):
            first = n * GROUP_TILES
            return x_all[:, first + tiles.start : first + tiles.stop, :].rearrange("p t (c e) -> p t c e", e=2)

        def add_b5(n, pair):
            planes = live["coupling", n][0]
            nc.vector.tensor_tensor(
                out=part(planes, pair).rearrange("p t e c -> p t (e c)"),
                in0=live["v", n, pair][:],
                in1=b5_planes[:].rearrange("p e c -> p (e c)").unsqueeze(1).to_broadcast([P, 2, WIDTH]),
                op=ALU.add,
            )

        def log_scale(n, tiles):
            planes, ls, scale, scaled = live["coupling", n]
            for t in tiles:
                tile_index = n * GROUP_TILES + t
                nc.scalar.activation(
                    out=ls[:, t, :],
                    in_=planes[:, t, 0, :],
                    func=ACT.Tanh,
                    accum_out=sums[:, tile_index : tile_index + 1],
                )

        def exponentiate(n, tiles):
            planes, ls, scale, scaled = live["coupling", n]
            nc.scalar.activation(out=part(scale, tiles), in_=part(ls, tiles), func=ACT.Exp)

        def scale_x(n, tiles):
            planes, ls, scale, scaled = live["coupling", n]
            nc.vector.tensor_tensor(
                out=part(scaled, tiles), in0=x_pairs(n, tiles)[:, :, :, 1], in1=part(scale, tiles), op=ALU.mult
            )

        def pass_x(n, copy):
            y_planes = stage.tile([P, GROUP_TILES, 2, HALF], F32, bufs=3)
            live["y_planes", n] = y_planes
            copy(out=y_planes[:, :, 0, :], in_=x_pairs(n, ALL)[:, :, :, 0])

        def shift_x(n, tiles):
            planes, ls, scale, scaled = live["coupling", n]
            nc.vector.tensor_tensor(
                out=part(live["y_planes", n], tiles)[:, :, 1, :],
                in0=part(planes, tiles)[:, :, 1, :],
                in1=part(scaled, tiles),
                op=ALU.add,
            )

        def copy_on_gpsimd(out, in_):
            nc.gpsimd.tensor_scalar(out=out, in0=in_, scalar1=1.0, scalar2=0.0, op0=ALU.mult, op1=ALU.add)

        def store_y(n, tiles, interleave):
            if tiles.start == 0:
                y = stage.tile([P, GROUP_TILES, HALF, 2], F32, bufs=3)
                live["y", n] = y
            y = live["y", n]
            interleave(out=part(y, tiles), in_=part(live["y_planes", n], tiles).rearrange("p t e c -> p t c e"))
            first = n * GROUP_TILES
            nc.sync.dma_start(
                out=y_rows[:, first + tiles.start : first + tiles.stop, :],
                in_=part(y, tiles).rearrange("p t c e -> p t (c e)"),
            )

        def on(k):
            return 0 <= k < GROUPS

        def one_round(n):
            if n > 0:
                first_matmul(n, 0)
            first_matmul(n, 1)
            if on(n - 1):
                regroup_h4(n - 1, 1)
            if on(n - 3):
                scale_x(n - 3, ALL)
            if on(n - 1):
                quantise_h4(n - 1)
            quantise_h3(n + 1)
            if on(n - 3):
                shift_x(n - 3, ALL)
            regroup_h4(n, 0)
            if n == 0:
                pack_w5()
            if n + 3 in SORTED_GROUPS and n == 1:
                sort_words(n + 3, nc.scalar.copy)
            if on(n - 1):
                second_matmul(n - 1)
            if on(n - 2):
                log_scale(n - 2, ALL)
                exponentiate(n - 2, ALL)
            if on(n + 2):
                transpose_h3(n + 2)
            if on(n - 3):
                store_y(n - 3, ALL, copy_on_gpsimd)
                pass_x(n - 2, copy_on_gpsimd)
            if on(n - 1):
                for pair in PAIRS:
                    add_b5(n - 1, pair)
            if on(n + 2):
                empty_vector_tiles(n + 2)
            if n + 3 in SORTED_GROUPS and n != 1:
                sort_words(n + 3, nc.vector.tensor_copy)

        def last_rounds():
            n = GROUPS - 1
            first_matmul(n, 0)
            regroup_h4(n - 1, 1)
            scale_x(n - 3, ALL)
            quantise_h4(n - 1)
            for rows in HALVES:
                first_matmul(n, 1, rows)
            second_matmul(n - 1)
            log_scale(n - 2, ALL)
            pass_x(n - 2, nc.scalar.copy)
            exponentiate(n - 2, ALL)
            regroup_h4(n, 0)
            shift_x(n - 3, ALL)
            store_y(n - 3, ALL, nc.scalar.copy)
            quantise_h4_part(n, 0)
            regroup_h4(n, 1, HALVES[0])
            add_b5(n - 1, PAIRS[0])
            quantise_h4_part(n, 1, HALVES[0])
            regroup_h4(n, 1, HALVES[1])
            add_b5(n - 1, PAIRS[1])
            quantise_h4_part(n, 1, HALVES[1])
            second_matmul(n)
            log_scale(n - 1, PAIRS[0])
            pass_x(n - 1, nc.scalar.copy)
            log_scale(n - 1, PAIRS[1])
            exponentiate(n - 1, ALL)
            scale_x(n - 2, ALL)
            add_b5(n, PAIRS[0])
            shift_x(n - 2, ALL)
            log_scale(n, PAIRS[0])
            exponentiate(n, PAIRS[0])
            store_y(n - 2, ALL, nc.scalar.copy)
            pass_x(n, nc.scalar.copy)
            scale_x(n - 1, ALL)
            add_b5(n, PAIRS[1])
            log_scale(n, PAIRS[1])
            exponentiate(n, PAIRS[1])
            shift_x(n - 1, ALL)
            scale_x(n, PAIRS[0])
            store_y(n - 1, ALL, nc.vector.tensor_copy)
            shift_x(n, PAIRS[0])
            scale_x(n, PAIRS[1])
            store_y(n, PAIRS[0], nc.vector.tensor_copy)
            shift_x(n, PAIRS[1])
            log_det = keep.tile([P, TILES], F32)
            nc.vector.tensor_tensor(out=log_det[:], in0=sums[:], in1=ldj[:], op=ALU.add)
            nc.sync.dma_start(out=out_1.rearrange("(p t) -> p t", t=TILES), in_=log_det[:])
            store_y(n, PAIRS[1], nc.vector.tensor_copy)

        pass_x(0, copy_on_gpsimd)
        warm_up(6)
        regroup_w4(0, 0)
        regroup_w4(0, 1)
        quantise_w4(0, 0)
        quantise_w4(0, 1)
        transpose_h3(0)
        h3_codes_of(0)
        quantise_first_h3(HALVES[0])
        first_matmul(0, 0, HALVES[0])
        quantise_first_h3(HALVES[1])
        first_matmul(0, 0, HALVES[1])
        transpose_h3(1)
        spread_b5()
        regroup_w4(1, 0)
        regroup_w4(1, 1)
        quantise_w4(1, 0)
        quantise_w4(1, 1)
        empty_vector_tiles(1)
        for n in range(GROUPS - 1):
            one_round(n)
        last_rounds()
